import numpy as np
import ml_dtypes


def mxq(x, axis, fmt="e4m3"):
    dtype, down = {"e4m3": (ml_dtypes.float8_e4m3fn, 7), "e5m2": (ml_dtypes.float8_e5m2, 14)}[fmt]
    v = np.moveaxis(np.asarray(x, np.float32).astype(ml_dtypes.bfloat16).astype(np.float64), axis, -1)
    blocks = v.reshape(v.shape[:-1] + (-1, 32))
    amax = np.abs(blocks).max(-1, keepdims=True)
    byte = np.maximum(np.where(amax > 0, np.frexp(amax)[1] - 1 + 127, 0) - down, 1)
    scale = np.exp2(byte - 127.0)
    codes = (blocks / scale).astype(np.float32).astype(dtype).astype(np.float64)
    return np.moveaxis((codes * scale).reshape(v.shape), -1, axis)


WIDE = False


def mx_kscale(k):
    if not WIDE:
        return np.ones(k)
    levels = np.array([10, -10, 5, -5, 0])
    a = np.random.permutation(np.resize(levels, k // 512 * 4)).reshape(k // 512, 4)
    idx = np.arange(k)
    return np.exp2(a[idx // 512, idx % 128 // 32])


BF16 = ml_dtypes.bfloat16


def bf(x):
    return np.asarray(x, np.float32).astype(BF16)


def f64(x):
    return np.asarray(x).astype(np.float64)


E2M1 = np.array([0.0, 0.5, 1.0, 1.5, 2.0, 3.0, 4.0, 6.0, -0.0, -0.5, -1.0, -1.5, -2.0, -3.0, -4.0, -6.0])


def pack_weight(w, fmt):
    k, n = w.shape
    w = f64(bf(w)).reshape(k // 32, 32, n)
    amax = np.abs(w).max(1)
    if fmt == "e4m3":
        byte = np.frexp(amax)[1] - 1 + 127 - 7
    else:
        mant, ex = np.frexp(amax / 6.0)
        byte = np.where(mant > 0.5, ex, ex - 1) + 127
    byte = np.clip(np.where(amax > 0, byte, 1), 1, 254)
    scaled = (w * np.exp2(127.0 - byte)[:, None, :]).reshape(k, n).astype(np.float32)
    by_word = np.ascontiguousarray(scaled.reshape(k // 512, 128, 4, n).transpose(0, 1, 3, 2))
    if fmt == "e4m3":
        words = by_word.astype(ml_dtypes.float8_e4m3fn).view(np.uint8)
    else:
        c = by_word.astype(ml_dtypes.float4_e2m1fn).view(np.uint8) & 0xF
        words = c[..., 0::2] | (c[..., 1::2] << 4)
    return np.ascontiguousarray(words), np.ascontiguousarray(byte.astype(np.uint8).reshape(k // 512, 16, n))


def unpack_weight(words, scales, fmt):
    g, p, n, _ = words.shape
    if fmt == "e4m3":
        vals = np.ascontiguousarray(words).view(ml_dtypes.float8_e4m3fn).astype(np.float64)
    else:
        nib = np.empty((g, p, n, 4), np.uint8)
        nib[..., 0::2] = words & 0xF
        nib[..., 1::2] = words >> 4
        vals = E2M1[nib]
    vals = vals * np.repeat(np.exp2(scales.astype(np.float64) - 127.0), 8, axis=1)[..., None]
    return vals.transpose(0, 1, 3, 2).reshape(g * 512, n)

def pack4(w):
    words, scales = pack_weight(w, "e2m1")
    return words.reshape(words.shape[0], 128, -1), scales


def unpack4(words, scales):
    return unpack_weight(words.reshape(words.shape[0], 128, -1, 2), scales, "e2m1")


B, T, D, H, HD = 4, 2048, 512, 2, 64
E = H * HD
HALF = HD // 2


def rotate_half(u):
    return np.concatenate((-u[..., HALF:], u[..., :HALF]), axis=-1)


def setup_inputs():
    s = mx_kscale(D)
    x = bf(np.random.standard_normal((B, T, D)) * s)
    rope_cos = bf(np.random.random_sample((1, 1, T, HD)))
    rope_sin = bf(np.random.random_sample((1, 1, T, HD)))
    w = np.random.standard_normal((3 * E, D)) / np.sqrt(D) / s[None, :]
    words, scales = pack4(np.ascontiguousarray(w.T))
    qkv_b = bf(np.random.standard_normal(3 * E) * 0.3)
    return {"x": x,
            "rope_cos": rope_cos,
            "rope_sin": rope_sin,
            "qkv_w_words": words,
            "qkv_w_scales": scales,
            "qkv_b": qkv_b}


def reference(x, rope_cos, rope_sin, qkv_w_words, qkv_w_scales, qkv_b):
    qkv = (mxq(f64(x), 2, "e4m3") @ unpack4(qkv_w_words, qkv_w_scales)) + f64(qkv_b)
    qkv = qkv.reshape(B, T, 3, H, HD).transpose(2, 0, 3, 1, 4)
    q, k, v = qkv[0], qkv[1], qkv[2]
    cos = f64(rope_cos)[:, :, :T, :]
    sin = f64(rope_sin)[:, :, :T, :]
    q_rot = q * cos + rotate_half(q) * sin
    k_rot = k * cos + rotate_half(k) * sin
    return q_rot, k_rot, v

@@ -1,0 +1,241 @@
+from contextlib import ExitStack
+
+import concourse.mybir as mybir
+from concourse.masks import make_identity
+
+F32 = mybir.dt.float32
+BF16 = mybir.dt.bfloat16
+I32 = mybir.dt.int32
+U32 = mybir.dt.uint32
+U8 = mybir.dt.uint8
+FP8X4 = mybir.dt.float8_e4m3fn_x4
+FP4X4 = mybir.dt.float4_e2m1fn_x4
+ALU = mybir.AluOpType
+ACT = mybir.ActivationFunctionType
+
+P = 128
+BATCH, SEQ, K = 4, 2048, 512
+HEADS, HEAD_DIM = 2, 64
+HALF = HEAD_DIM // 2
+PAIRS = 2 * HEADS
+FEATURES = 3 * HEADS * HEAD_DIM
+OPERANDS = FEATURES // P
+LOW, HIGH, VALUE = 0, 1, 2
+TOKENS_PER_PARTITION = SEQ // P
+TILES = 4
+ROUND_TOKENS = TILES * P
+ROUNDS_PER_BATCH = TOKENS_PER_PARTITION // TILES
+ROUNDS = BATCH * ROUNDS_PER_BATCH
+WORDS = K // 2
+
+FLOPS = 2 * BATCH * SEQ * K * FEATURES
+
+
+def regroup_columns(nc, dst, src, width):
+    rotated = 2 * PAIRS * width
+    nc.vector.tensor_copy(
+        out=dst[:, 0:rotated].rearrange("p (f g i) -> p f g i", f=2, g=PAIRS),
+        in_=src[:, 0:rotated].rearrange("p (g f i) -> p f g i", g=PAIRS, f=2),
+    )
+    nc.vector.tensor_copy(out=dst[:, rotated:], in_=src[:, rotated:])
+
+
+def tile_causalselfattention_pa_t_kernel(
+    tc, x, rope_cos, rope_sin, qkv_w_words, qkv_w_scales, qkv_b, out_0, out_1, out_2
+):
+    nc = tc.nc
+    with ExitStack() as ctx:
+        ctx.enter_context(tc.manual_schedule())
+        const = ctx.enter_context(tc.tile_pool(name="const", bufs=1))
+        x_pool = ctx.enter_context(tc.tile_pool(name="x", bufs=ROUNDS))
+        quant_pool = ctx.enter_context(tc.tile_pool(name="quant", bufs=2))
+        feat_pool = ctx.enter_context(tc.tile_pool(name="feat", bufs=2 * OPERANDS))
+        prod_pool = ctx.enter_context(tc.tile_pool(name="prod", bufs=2))
+        out_pool = ctx.enter_context(tc.tile_pool(name="out", bufs=3))
+        psum_xt = ctx.enter_context(tc.psum_pool(name="psum_xt", bufs=2))
+        psum_acc = ctx.enter_context(tc.psum_pool(name="psum_acc", bufs=OPERANDS))
+        psum_tok = ctx.enter_context(tc.psum_pool(name="psum_tok", bufs=OPERANDS))
+
+        def round_place(r):
+            b, jq = divmod(r, ROUNDS_PER_BATCH)
+            return b, slice(TILES * jq, TILES * (jq + 1))
+
+        x_tiles = []
+
+        def load_x(r):
+            b, places = round_place(r)
+            x_sb = x_pool.tile([P, TILES, K], BF16)
+            rows = x[b].rearrange("(p j) k -> p j k", j=TOKENS_PER_PARTITION)
+            nc.sync.dma_start(out=x_sb[:], in_=rows[:, places, :])
+            x_tiles.append(x_sb)
+
+        load_x(0)
+
+        w_words_in = const.tile([P, 2 * FEATURES], U8)
+        nc.sync.dma_start(out=w_words_in[:].bitcast(I32), in_=qkv_w_words[0].bitcast(I32))
+        w_scales_in = const.tile([P, FEATURES], U8)
+        nc.vector.memset(w_scales_in[:].bitcast(I32), 0)
+        for quadrant in range(4):
+            nc.sync.dma_start(
+                out=w_scales_in[32 * quadrant : 32 * quadrant + 4, :].bitcast(I32),
+                in_=qkv_w_scales[0, 4 * quadrant : 4 * quadrant + 4, :].bitcast(I32),
+            )
+        load_x(1)
+
+        bias_rows = const.tile([P, P], BF16)
+        nc.vector.memset(bias_rows[:], 0.0)
+        nc.scalar.dma_start(
+            out=bias_rows[LOW : HIGH + 1, :].rearrange("f (g i) -> f g i", g=PAIRS),
+            in_=qkv_b[0 : 2 * P].rearrange("(g f i) -> f g i", g=PAIRS, f=2),
+        )
+        nc.scalar.dma_start(
+            out=bias_rows[VALUE : VALUE + 1, :],
+            in_=qkv_b[2 * P : 3 * P].rearrange("(o c) -> o c", o=1),
+        )
+        cos_sb = const.tile([P, TOKENS_PER_PARTITION, HEAD_DIM], BF16)
+        sin_sb = const.tile([P, TOKENS_PER_PARTITION, HEAD_DIM], BF16)
+        nc.scalar.dma_start(
+            out=cos_sb[:], in_=rope_cos[0, 0].rearrange("(p j) d -> p j d", j=TOKENS_PER_PARTITION)
+        )
+        nc.scalar.dma_start(
+            out=sin_sb[:], in_=rope_sin[0, 0].rearrange("(p j) d -> p j d", j=TOKENS_PER_PARTITION)
+        )
+        for r in range(2, ROUNDS):
+            load_x(r)
+
+        identity = const.tile([P, P], F32)
+        make_identity(nc, identity[:])
+
+        w_words = const.tile([P, OPERANDS, 2 * P], U8, align_bytes=64)
+        w_scales = const.tile([P, OPERANDS, P], U8, align_bytes=64)
+        regroup_columns(
+            nc,
+            w_words[:].rearrange("p s c -> p (s c)").bitcast(I32),
+            w_words_in[:].bitcast(I32),
+            2 * HALF // 4,
+        )
+        regroup_columns(
+            nc,
+            w_scales[:].rearrange("p s c -> p (s c)").bitcast(I32),
+            w_scales_in[:].bitcast(I32),
+            HALF // 4,
+        )
+
+        bias_rows_f32 = const.tile([P, P], F32)
+        nc.vector.tensor_copy(out=bias_rows_f32[:], in_=bias_rows[:])
+        bias_bank = psum_xt.tile([P, P], F32, tag="xt")
+        nc.tensor.transpose(out=bias_bank[:], in_=bias_rows_f32[:], identity=identity[:])
+        bias = const.tile([P, OPERANDS], F32)
+        nc.vector.tensor_copy(out=bias[:], in_=bias_bank[:, 0:OPERANDS])
+
+        x_codes = {}
+        x_scales = {}
+
+        def transpose_and_quantise(r):
+            x_words = x_tiles[r][:].bitcast(F32)
+            grouped = quant_pool.tile([P, 4 * ROUND_TOKENS], BF16, align_bytes=64)
+            grouped_words = grouped[:].bitcast(F32)
+            for half_round in range(2):
+                xt = psum_xt.tile([P, 2, 2 * P], F32, tag="xt")
+                for tile_in_bank in range(2):
+                    jj = 2 * half_round + tile_in_bank
+                    for parity in range(2):
+                        nc.tensor.transpose(
+                            out=xt[:, parity, P * tile_in_bank : P * (tile_in_bank + 1)],
+                            in_=x_words[:, jj, parity:WORDS:2],
+                            identity=identity[:],
+                        )
+                nc.scalar.copy(
+                    out=grouped_words[:, 4 * P * half_round : 4 * P * (half_round + 1)].rearrange(
+                        "p (n u) -> p n u", u=2
+                    ),
+                    in_=xt[:].rearrange("p u n -> p n u"),
+                )
+            codes = quant_pool.tile([P, ROUND_TOKENS], U32, align_bytes=64)
+            scales = quant_pool.tile([P, ROUND_TOKENS], U8, align_bytes=64)
+            nc.vector.quantize_mx(out=codes[:].bitcast(FP8X4), scales=scales[:], in_=grouped[:])
+            x_codes[r] = codes
+            x_scales[r] = scales
+
+        features = {}
+
+        def project(r):
+            for s in range(OPERANDS):
+                acc = psum_acc.tile([P, ROUND_TOKENS], F32)
+                nc.tensor.matmul_mx(
+                    out=acc[:],
+                    lhsT=w_words[:, s, :].bitcast(FP4X4),
+                    lhsT_scale=w_scales[:, s, :],
+                    rhs=x_codes[r][:].bitcast(FP8X4),
+                    rhs_scale=x_scales[r][:],
+                    start=True,
+                    stop=True,
+                )
+                feat = feat_pool.tile([P, ROUND_TOKENS], F32)
+                nc.scalar.activation(
+                    out=feat[:], in_=acc[:], func=ACT.Identity, bias=bias[:, s : s + 1], scale=1.0
+                )
+                features[(r, s)] = feat
+
+        def rotate_and_store(r):
+            b, places = round_place(r)
+            banks = []
+            for s in range(OPERANDS):
+                tok = psum_tok.tile([P, TILES, P], F32)
+                for jj in range(TILES):
+                    nc.tensor.transpose(
+                        out=tok[:, jj, :],
+                        in_=features[(r, s)][:, P * jj : P * (jj + 1)],
+                        identity=identity[:],
+                    )
+                banks.append(tok)
+            low = banks[LOW][:].rearrange("p j (g i) -> p j g i", g=PAIRS)
+            high = banks[HIGH][:].rearrange("p j (g i) -> p j g i", g=PAIRS)
+
+            def table(sb, first):
+                part = sb[:, places, first : first + HALF]
+                return part.unsqueeze(2).to_broadcast([P, TILES, PAIRS, HALF])
+
+            low_cos = prod_pool.tile([P, TILES, PAIRS, HALF], F32)
+            low_sin = prod_pool.tile([P, TILES, PAIRS, HALF], F32)
+            high_sin = prod_pool.tile([P, TILES, PAIRS, HALF], F32)
+            high_cos = prod_pool.tile([P, TILES, PAIRS, HALF], F32)
+            nc.vector.tensor_tensor(out=low_cos[:], in0=low, in1=table(cos_sb, 0), op=ALU.mult)
+            nc.vector.tensor_tensor(out=low_sin[:], in0=low, in1=table(sin_sb, HALF), op=ALU.mult)
+            nc.vector.tensor_tensor(out=high_sin[:], in0=high, in1=table(sin_sb, 0), op=ALU.mult)
+            nc.vector.tensor_tensor(out=high_cos[:], in0=high, in1=table(cos_sb, HALF), op=ALU.mult)
+
+            rotated = out_pool.tile([P, PAIRS, TILES, HEAD_DIM], F32)
+            nc.gpsimd.tensor_tensor(
+                out=rotated[:, :, :, 0:HALF].rearrange("p g j i -> p j g i"),
+                in0=low_cos[:],
+                in1=high_sin[:],
+                op=ALU.subtract,
+            )
+            nc.gpsimd.tensor_tensor(
+                out=rotated[:, :, :, HALF:HEAD_DIM].rearrange("p g j i -> p j g i"),
+                in0=high_cos[:],
+                in1=low_sin[:],
+                op=ALU.add,
+            )
+            value = out_pool.tile([P, HEADS, TILES, HEAD_DIM], F32)
+            nc.scalar.copy(
+                out=value[:].rearrange("p h j d -> p j h d"),
+                in_=banks[VALUE][:].rearrange("p j (h d) -> p j h d", h=HEADS),
+            )
+
+            def place_in(out):
+                rows = out[b].rearrange("h (p j) d -> p h j d", j=TOKENS_PER_PARTITION)
+                return rows[:, :, places, :]
+
+            nc.sync.dma_start(out=place_in(out_2), in_=value[:])
+            nc.sync.dma_start(out=place_in(out_0), in_=rotated[:, 0:HEADS])
+            nc.sync.dma_start(out=place_in(out_1), in_=rotated[:, HEADS:PAIRS])
+
+        for step in range(ROUNDS + 2):
+            if step < ROUNDS:
+                transpose_and_quantise(step)
+            if 1 <= step <= ROUNDS:
+                project(step - 1)
+            if step >= 2:
+                rotate_and_store(step - 2)

@@ -65,8 +65,9 @@ def tile_causalselfattention_pa_t_kernel(
         def load_x(r):
             b, places = round_place(r)
             x_sb = x_pool.tile([P, TILES, K], BF16)
-            rows = x[b].rearrange("(p j) k -> p j k", j=TOKENS_PER_PARTITION)
-            nc.sync.dma_start(out=x_sb[:], in_=rows[:, places, :])
+            rows = x[b].rearrange("(p j) k -> p j k", j=TOKENS_PER_PARTITION)[:, places, :]
+            for first in range(0, TILES, 2):
+                nc.sync.dma_start(out=x_sb[:, first : first + 2, :], in_=rows[:, first : first + 2, :])
             x_tiles.append(x_sb)
 
         load_x(0)
@@ -123,10 +124,12 @@ def tile_causalselfattention_pa_t_kernel(
 
         bias_rows_f32 = const.tile([P, P], F32)
         nc.vector.tensor_copy(out=bias_rows_f32[:], in_=bias_rows[:])
-        bias_bank = psum_xt.tile([P, P], F32, tag="xt")
-        nc.tensor.transpose(out=bias_bank[:], in_=bias_rows_f32[:], identity=identity[:])
         bias = const.tile([P, OPERANDS], F32)
-        nc.vector.tensor_copy(out=bias[:], in_=bias_bank[:, 0:OPERANDS])
+
+        def bias_onto_partitions():
+            bias_bank = psum_tok.tile([P, P], F32, tag="tok")
+            nc.tensor.transpose(out=bias_bank[:], in_=bias_rows_f32[:], identity=identity[:])
+            nc.vector.tensor_copy(out=bias[:], in_=bias_bank[:, 0:OPERANDS])
 
         x_codes = {}
         x_scales = {}
@@ -219,7 +222,8 @@ def tile_causalselfattention_pa_t_kernel(
                 op=ALU.add,
             )
             value = out_pool.tile([P, HEADS, TILES, HEAD_DIM], F32)
-            nc.scalar.copy(
+            copy_out = nc.scalar.copy if r % 2 == 0 else nc.vector.tensor_copy
+            copy_out(
                 out=value[:].rearrange("p h j d -> p j h d"),
                 in_=banks[VALUE][:].rearrange("p j (h d) -> p j h d", h=HEADS),
             )
@@ -235,6 +239,8 @@ def tile_causalselfattention_pa_t_kernel(
         for step in range(ROUNDS + 2):
             if step < ROUNDS:
                 transpose_and_quantise(step)
+            if step == 0:
+                bias_onto_partitions()
             if 1 <= step <= ROUNDS:
                 project(step - 1)
             if step >= 2:

@@ -54,7 +54,7 @@ def tile_causalselfattention_pa_t_kernel(
         out_pool = ctx.enter_context(tc.tile_pool(name="out", bufs=3))
         psum_xt = ctx.enter_context(tc.psum_pool(name="psum_xt", bufs=2))
         psum_acc = ctx.enter_context(tc.psum_pool(name="psum_acc", bufs=OPERANDS))
-        psum_tok = ctx.enter_context(tc.psum_pool(name="psum_tok", bufs=OPERANDS))
+        psum_tok = ctx.enter_context(tc.psum_pool(name="psum_tok", bufs=1))
 
         def round_place(r):
             b, jq = divmod(r, ROUNDS_PER_BATCH)
@@ -104,6 +104,13 @@ def tile_causalselfattention_pa_t_kernel(
         for r in range(2, ROUNDS):
             load_x(r)
 
+        minus_sin_low = const.tile([P, TOKENS_PER_PARTITION, HALF], BF16)
+
+        def negate_sin():
+            nc.vector.tensor_scalar(
+                out=minus_sin_low[:], in0=sin_sb[:, :, 0:HALF], scalar1=-1.0, scalar2=None, op0=ALU.mult
+            )
+
         identity = const.tile([P, P], F32)
         make_identity(nc, identity[:])
 
@@ -127,36 +134,42 @@ def tile_causalselfattention_pa_t_kernel(
         bias = const.tile([P, OPERANDS], F32)
 
         def bias_onto_partitions():
-            bias_bank = psum_tok.tile([P, P], F32, tag="tok")
+            bias_bank = psum_tok.tile([P, P], F32, tag="tok_value")
             nc.tensor.transpose(out=bias_bank[:], in_=bias_rows_f32[:], identity=identity[:])
             nc.vector.tensor_copy(out=bias[:], in_=bias_bank[:, 0:OPERANDS])
 
+        grouped_tiles = {}
         x_codes = {}
         x_scales = {}
 
-        def transpose_and_quantise(r):
+        def transpose_x(r, half_round):
+            if half_round == 0:
+                grouped_new = quant_pool.tile([P, 4 * ROUND_TOKENS], BF16, align_bytes=64, tag="grouped")
+                grouped_tiles[r] = grouped_new
             x_words = x_tiles[r][:].bitcast(F32)
-            grouped = quant_pool.tile([P, 4 * ROUND_TOKENS], BF16, align_bytes=64)
-            grouped_words = grouped[:].bitcast(F32)
-            for half_round in range(2):
-                xt = psum_xt.tile([P, 2, 2 * P], F32, tag="xt")
-                for tile_in_bank in range(2):
-                    jj = 2 * half_round + tile_in_bank
-                    for parity in range(2):
-                        nc.tensor.transpose(
-                            out=xt[:, parity, P * tile_in_bank : P * (tile_in_bank + 1)],
-                            in_=x_words[:, jj, parity:WORDS:2],
-                            identity=identity[:],
-                        )
-                nc.scalar.copy(
-                    out=grouped_words[:, 4 * P * half_round : 4 * P * (half_round + 1)].rearrange(
-                        "p (n u) -> p n u", u=2
-                    ),
-                    in_=xt[:].rearrange("p u n -> p n u"),
-                )
-            codes = quant_pool.tile([P, ROUND_TOKENS], U32, align_bytes=64)
-            scales = quant_pool.tile([P, ROUND_TOKENS], U8, align_bytes=64)
-            nc.vector.quantize_mx(out=codes[:].bitcast(FP8X4), scales=scales[:], in_=grouped[:])
+            grouped_words = grouped_tiles[r][:].bitcast(F32)
+            xt = psum_xt.tile([P, 2, 2 * P], F32, tag="xt")
+            for tile_in_bank in range(2):
+                jj = 2 * half_round + tile_in_bank
+                for parity in range(2):
+                    nc.tensor.transpose(
+                        out=xt[:, parity, P * tile_in_bank : P * (tile_in_bank + 1)],
+                        in_=x_words[:, jj, parity:WORDS:2],
+                        identity=identity[:],
+                    )
+            nc.scalar.copy(
+                out=grouped_words[:, 4 * P * half_round : 4 * P * (half_round + 1)].rearrange(
+                    "p (n u) -> p n u", u=2
+                ),
+                in_=xt[:].rearrange("p u n -> p n u"),
+            )
+
+        def quantise(r):
+            codes = quant_pool.tile([P, ROUND_TOKENS], U32, align_bytes=64, tag="codes")
+            scales = quant_pool.tile([P, ROUND_TOKENS], U8, align_bytes=64, tag="scales")
+            nc.vector.quantize_mx(
+                out=codes[:].bitcast(FP8X4), scales=scales[:], in_=grouped_tiles[r][:]
+            )
             x_codes[r] = codes
             x_scales[r] = scales
 
@@ -164,7 +177,7 @@ def tile_causalselfattention_pa_t_kernel(
 
         def project(r):
             for s in range(OPERANDS):
-                acc = psum_acc.tile([P, ROUND_TOKENS], F32)
+                acc = psum_acc.tile([P, ROUND_TOKENS], F32, tag="acc")
                 nc.tensor.matmul_mx(
                     out=acc[:],
                     lhsT=w_words[:, s, :].bitcast(FP4X4),
@@ -174,74 +187,130 @@ def tile_causalselfattention_pa_t_kernel(
                     start=True,
                     stop=True,
                 )
-                feat = feat_pool.tile([P, ROUND_TOKENS], F32)
+                feat = feat_pool.tile([P, ROUND_TOKENS], F32, tag="feat")
                 nc.scalar.activation(
                     out=feat[:], in_=acc[:], func=ACT.Identity, bias=bias[:, s : s + 1], scale=1.0
                 )
                 features[(r, s)] = feat
 
-        def rotate_and_store(r):
-            b, places = round_place(r)
-            banks = []
-            for s in range(OPERANDS):
-                tok = psum_tok.tile([P, TILES, P], F32)
-                for jj in range(TILES):
+        FIRST, SECOND = 0, 1
+        banks = {}
+        prod_cos = {}
+        prod_sin = {}
+        rotated_tiles = {}
+
+        def back_rotated(r, part):
+            tok = psum_tok.tile([P, 2, 2, P], F32, tag="tok_first" if part == FIRST else "tok_second")
+            for j in range(2):
+                jj = 2 * part + j
+                for s in (LOW, HIGH):
                     nc.tensor.transpose(
-                        out=tok[:, jj, :],
+                        out=tok[:, j, s, :],
                         in_=features[(r, s)][:, P * jj : P * (jj + 1)],
                         identity=identity[:],
                     )
-                banks.append(tok)
-            low = banks[LOW][:].rearrange("p j (g i) -> p j g i", g=PAIRS)
-            high = banks[HIGH][:].rearrange("p j (g i) -> p j g i", g=PAIRS)
+            banks[(r, part)] = tok
 
-            def table(sb, first):
-                part = sb[:, places, first : first + HALF]
-                return part.unsqueeze(2).to_broadcast([P, TILES, PAIRS, HALF])
+        def part_places(r, part):
+            b, jq = divmod(r, ROUNDS_PER_BATCH)
+            first = TILES * jq + 2 * part
+            return slice(first, first + 2)
 
-            low_cos = prod_pool.tile([P, TILES, PAIRS, HALF], F32)
-            low_sin = prod_pool.tile([P, TILES, PAIRS, HALF], F32)
-            high_sin = prod_pool.tile([P, TILES, PAIRS, HALF], F32)
-            high_cos = prod_pool.tile([P, TILES, PAIRS, HALF], F32)
-            nc.vector.tensor_tensor(out=low_cos[:], in0=low, in1=table(cos_sb, 0), op=ALU.mult)
-            nc.vector.tensor_tensor(out=low_sin[:], in0=low, in1=table(sin_sb, HALF), op=ALU.mult)
-            nc.vector.tensor_tensor(out=high_sin[:], in0=high, in1=table(sin_sb, 0), op=ALU.mult)
-            nc.vector.tensor_tensor(out=high_cos[:], in0=high, in1=table(cos_sb, HALF), op=ALU.mult)
-
-            rotated = out_pool.tile([P, PAIRS, TILES, HEAD_DIM], F32)
-            nc.gpsimd.tensor_tensor(
-                out=rotated[:, :, :, 0:HALF].rearrange("p g j i -> p j g i"),
-                in0=low_cos[:],
-                in1=high_sin[:],
-                op=ALU.subtract,
+        def times_cos(r, part):
+            places = part_places(r, part)
+            name = "cos_first" if part == FIRST else "cos_second"
+            prod = prod_pool.tile([P, PAIRS, 2, HEAD_DIM], F32, tag=name)
+            table = cos_sb[:, places, :].rearrange("p j (f i) -> p (j f) i", f=2)
+            nc.vector.tensor_tensor(
+                out=prod[:].rearrange("p g j (f i) -> p (j f) g i", f=2),
+                in0=banks[(r, part)][:].rearrange("p j f (g i) -> p (j f) g i", g=PAIRS),
+                in1=table.unsqueeze(2).to_broadcast([P, 4, PAIRS, HALF]),
+                op=ALU.mult,
             )
-            nc.gpsimd.tensor_tensor(
-                out=rotated[:, :, :, HALF:HEAD_DIM].rearrange("p g j i -> p j g i"),
-                in0=high_cos[:],
-                in1=low_sin[:],
+            prod_cos[(r, part)] = prod
+
+        def times_sin(r, part, source):
+            places = part_places(r, part)
+            if source == LOW:
+                name = "sin_first" if part == FIRST else "sin_second"
+                prod_new = prod_pool.tile([P, PAIRS, 2, HEAD_DIM], F32, tag=name)
+                prod_sin[(r, part)] = prod_new
+                table = sin_sb[:, places, HALF:HEAD_DIM]
+                target = prod_sin[(r, part)][:, :, :, HALF:HEAD_DIM]
+            else:
+                table = minus_sin_low[:, places, :]
+                target = prod_sin[(r, part)][:, :, :, 0:HALF]
+            nc.vector.tensor_tensor(
+                out=target.rearrange("p g j i -> p j g i"),
+                in0=banks[(r, part)][:, :, source, :].rearrange("p j (g i) -> p j g i", g=PAIRS),
+                in1=table.unsqueeze(2).to_broadcast([P, 2, PAIRS, HALF]),
+                op=ALU.mult,
+            )
+
+        def add_products(r, part, engine):
+            if part == FIRST:
+                rotated_new = out_pool.tile([P, PAIRS, TILES, HEAD_DIM], F32, tag="rotated")
+                rotated_tiles[r] = rotated_new
+            engine.tensor_tensor(
+                out=rotated_tiles[r][:, :, 2 * part : 2 * part + 2, :].rearrange("p g j d -> p g (j d)"),
+                in0=prod_cos[(r, part)][:].rearrange("p g j d -> p g (j d)"),
+                in1=prod_sin[(r, part)][:].rearrange("p g j d -> p g (j d)"),
                 op=ALU.add,
             )
-            value = out_pool.tile([P, HEADS, TILES, HEAD_DIM], F32)
-            copy_out = nc.scalar.copy if r % 2 == 0 else nc.vector.tensor_copy
-            copy_out(
+
+        def place_in(out, r):
+            b, places = round_place(r)
+            rows = out[b].rearrange("h (p j) d -> p h j d", j=TOKENS_PER_PARTITION)
+            return rows[:, :, places, :]
+
+        def store_rotated(r):
+            nc.sync.dma_start(out=place_in(out_0, r), in_=rotated_tiles[r][:, 0:HEADS])
+            nc.sync.dma_start(out=place_in(out_1, r), in_=rotated_tiles[r][:, HEADS:PAIRS])
+
+        def back_value_and_store(r):
+            tok = psum_tok.tile([P, TILES, P], F32, tag="tok_value")
+            for jj in range(TILES):
+                nc.tensor.transpose(
+                    out=tok[:, jj, :],
+                    in_=features[(r, VALUE)][:, P * jj : P * (jj + 1)],
+                    identity=identity[:],
+                )
+            value = out_pool.tile([P, HEADS, TILES, HEAD_DIM], F32, tag="value")
+            nc.scalar.copy(
                 out=value[:].rearrange("p h j d -> p j h d"),
-                in_=banks[VALUE][:].rearrange("p j (h d) -> p j h d", h=HEADS),
+                in_=tok[:].rearrange("p j (h d) -> p j h d", h=HEADS),
             )
+            nc.sync.dma_start(out=place_in(out_2, r), in_=value[:])
 
-            def place_in(out):
-                rows = out[b].rearrange("h (p j) d -> p h j d", j=TOKENS_PER_PARTITION)
-                return rows[:, :, places, :]
+        def live(r):
+            return 0 <= r < ROUNDS
 
-            nc.sync.dma_start(out=place_in(out_2), in_=value[:])
-            nc.sync.dma_start(out=place_in(out_0), in_=rotated[:, 0:HEADS])
-            nc.sync.dma_start(out=place_in(out_1), in_=rotated[:, HEADS:PAIRS])
-
-        for step in range(ROUNDS + 2):
-            if step < ROUNDS:
-                transpose_and_quantise(step)
-            if step == 0:
+        for m in range(-3, ROUNDS + 1):
+            if live(m + 1):
+                project(m + 1)
+            if live(m):
+                times_cos(m, FIRST)
+                times_sin(m, FIRST, LOW)
+            if live(m - 1):
+                add_products(m - 1, SECOND, nc.vector)
+                store_rotated(m - 1)
+            if live(m + 2):
+                quantise(m + 2)
+            if m == -2:
+                negate_sin()
+            if live(m):
+                times_sin(m, FIRST, HIGH)
+                add_products(m, FIRST, nc.gpsimd)
+                back_rotated(m, SECOND)
+                back_value_and_store(m)
+            if live(m + 3):
+                transpose_x(m + 3, 0)
+                transpose_x(m + 3, 1)
+            if m == -3:
                 bias_onto_partitions()
-            if 1 <= step <= ROUNDS:
-                project(step - 1)
-            if step >= 2:
-                rotate_and_store(step - 2)
+            if live(m + 1):
+                back_rotated(m + 1, FIRST)
+            if live(m):
+                times_cos(m, SECOND)
+                times_sin(m, SECOND, LOW)
+                times_sin(m, SECOND, HIGH)

@@ -175,8 +175,8 @@ def tile_causalselfattention_pa_t_kernel(
 
         features = {}
 
-        def project(r):
-            for s in range(OPERANDS):
+        def project(r, operands):
+            for s in operands:
                 acc = psum_acc.tile([P, ROUND_TOKENS], F32, tag="acc")
                 nc.tensor.matmul_mx(
                     out=acc[:],
@@ -287,7 +287,7 @@ def tile_causalselfattention_pa_t_kernel(
 
         for m in range(-3, ROUNDS + 1):
             if live(m + 1):
-                project(m + 1)
+                project(m + 1, (LOW, HIGH))
             if live(m):
                 times_cos(m, FIRST)
                 times_sin(m, FIRST, LOW)
@@ -305,11 +305,13 @@ def tile_causalselfattention_pa_t_kernel(
                 back_value_and_store(m)
             if live(m + 3):
                 transpose_x(m + 3, 0)
+            if live(m + 1):
+                project(m + 1, (VALUE,))
+                back_rotated(m + 1, FIRST)
+            if live(m + 3):
                 transpose_x(m + 3, 1)
             if m == -3:
                 bias_onto_partitions()
-            if live(m + 1):
-                back_rotated(m + 1, FIRST)
             if live(m):
                 times_cos(m, SECOND)
                 times_sin(m, SECOND, LOW)

@@ -51,7 +51,7 @@ def tile_causalselfattention_pa_t_kernel(
         quant_pool = ctx.enter_context(tc.tile_pool(name="quant", bufs=2))
         feat_pool = ctx.enter_context(tc.tile_pool(name="feat", bufs=2 * OPERANDS))
         prod_pool = ctx.enter_context(tc.tile_pool(name="prod", bufs=2))
-        out_pool = ctx.enter_context(tc.tile_pool(name="out", bufs=3))
+        out_pool = ctx.enter_context(tc.tile_pool(name="out", bufs=8))
         psum_xt = ctx.enter_context(tc.psum_pool(name="psum_xt", bufs=2))
         psum_acc = ctx.enter_context(tc.psum_pool(name="psum_acc", bufs=OPERANDS))
         psum_tok = ctx.enter_context(tc.psum_pool(name="psum_tok", bufs=1))

@@ -49,6 +49,7 @@ def tile_causalselfattention_pa_t_kernel(
         const = ctx.enter_context(tc.tile_pool(name="const", bufs=1))
         x_pool = ctx.enter_context(tc.tile_pool(name="x", bufs=ROUNDS))
         quant_pool = ctx.enter_context(tc.tile_pool(name="quant", bufs=2))
+        grouped_pool = ctx.enter_context(tc.tile_pool(name="grouped", bufs=3))
         feat_pool = ctx.enter_context(tc.tile_pool(name="feat", bufs=2 * OPERANDS))
         prod_pool = ctx.enter_context(tc.tile_pool(name="prod", bufs=2))
         out_pool = ctx.enter_context(tc.tile_pool(name="out", bufs=8))
@@ -144,7 +145,7 @@ def tile_causalselfattention_pa_t_kernel(
 
         def transpose_x(r, half_round):
             if half_round == 0:
-                grouped_new = quant_pool.tile([P, 4 * ROUND_TOKENS], BF16, align_bytes=64, tag="grouped")
+                grouped_new = grouped_pool.tile([P, 4 * ROUND_TOKENS], BF16, align_bytes=64, tag="grouped")
                 grouped_tiles[r] = grouped_new
             x_words = x_tiles[r][:].bitcast(F32)
             grouped_words = grouped_tiles[r][:].bitcast(F32)
@@ -218,28 +219,29 @@ def tile_causalselfattention_pa_t_kernel(
 
         def times_cos(r, part):
             places = part_places(r, part)
-            name = "cos_first" if part == FIRST else "cos_second"
-            prod = prod_pool.tile([P, PAIRS, 2, HEAD_DIM], F32, tag=name)
+            if part == FIRST:
+                prod_new = prod_pool.tile([P, PAIRS, TILES, HEAD_DIM], F32, tag="prod_cos")
+                prod_cos[r] = prod_new
             table = cos_sb[:, places, :].rearrange("p j (f i) -> p (j f) i", f=2)
             nc.vector.tensor_tensor(
-                out=prod[:].rearrange("p g j (f i) -> p (j f) g i", f=2),
+                out=prod_cos[r][:, :, 2 * part : 2 * part + 2, :].rearrange("p g j (f i) -> p (j f) g i", f=2),
                 in0=banks[(r, part)][:].rearrange("p j f (g i) -> p (j f) g i", g=PAIRS),
                 in1=table.unsqueeze(2).to_broadcast([P, 4, PAIRS, HALF]),
                 op=ALU.mult,
             )
-            prod_cos[(r, part)] = prod
 
         def times_sin(r, part, source):
             places = part_places(r, part)
+            if source == LOW and part == FIRST:
+                prod_new = prod_pool.tile([P, PAIRS, TILES, HEAD_DIM], F32, tag="prod_sin")
+                prod_sin[r] = prod_new
+            tiles = slice(2 * part, 2 * part + 2)
             if source == LOW:
-                name = "sin_first" if part == FIRST else "sin_second"
-                prod_new = prod_pool.tile([P, PAIRS, 2, HEAD_DIM], F32, tag=name)
-                prod_sin[(r, part)] = prod_new
                 table = sin_sb[:, places, HALF:HEAD_DIM]
-                target = prod_sin[(r, part)][:, :, :, HALF:HEAD_DIM]
+                target = prod_sin[r][:, :, tiles, HALF:HEAD_DIM]
             else:
                 table = minus_sin_low[:, places, :]
-                target = prod_sin[(r, part)][:, :, :, 0:HALF]
+                target = prod_sin[r][:, :, tiles, 0:HALF]
             nc.vector.tensor_tensor(
                 out=target.rearrange("p g j i -> p j g i"),
                 in0=banks[(r, part)][:, :, source, :].rearrange("p j (g i) -> p j g i", g=PAIRS),
@@ -247,14 +249,15 @@ def tile_causalselfattention_pa_t_kernel(
                 op=ALU.mult,
             )
 
-        def add_products(r, part, engine):
-            if part == FIRST:
+        def add_products(r, first_tile, tiles, engine):
+            if first_tile == 0:
                 rotated_new = out_pool.tile([P, PAIRS, TILES, HEAD_DIM], F32, tag="rotated")
                 rotated_tiles[r] = rotated_new
+            chosen = slice(first_tile, first_tile + tiles)
             engine.tensor_tensor(
-                out=rotated_tiles[r][:, :, 2 * part : 2 * part + 2, :].rearrange("p g j d -> p g (j d)"),
-                in0=prod_cos[(r, part)][:].rearrange("p g j d -> p g (j d)"),
-                in1=prod_sin[(r, part)][:].rearrange("p g j d -> p g (j d)"),
+                out=rotated_tiles[r][:, :, chosen, :].rearrange("p g j d -> p g (j d)"),
+                in0=prod_cos[r][:, :, chosen, :].rearrange("p g j d -> p g (j d)"),
+                in1=prod_sin[r][:, :, chosen, :].rearrange("p g j d -> p g (j d)"),
                 op=ALU.add,
             )
 
@@ -276,43 +279,45 @@ def tile_causalselfattention_pa_t_kernel(
                     identity=identity[:],
                 )
             value = out_pool.tile([P, HEADS, TILES, HEAD_DIM], F32, tag="value")
-            nc.scalar.copy(
-                out=value[:].rearrange("p h j d -> p j h d"),
-                in_=tok[:].rearrange("p j (h d) -> p j h d", h=HEADS),
-            )
+            for copy_out, tiles in ((nc.scalar.copy, slice(0, 2)), (nc.vector.tensor_copy, slice(2, 4))):
+                copy_out(
+                    out=value[:, :, tiles, :].rearrange("p h j d -> p j h d"),
+                    in_=tok[:, tiles, :].rearrange("p j (h d) -> p j h d", h=HEADS),
+                )
             nc.sync.dma_start(out=place_in(out_2, r), in_=value[:])
 
         def live(r):
             return 0 <= r < ROUNDS
 
-        for m in range(-3, ROUNDS + 1):
+        last = ROUNDS - 1
+        for m in range(-3, ROUNDS):
             if live(m + 1):
-                project(m + 1, (LOW, HIGH))
+                quantise(m + 1)
+            if m == -1:
+                negate_sin()
             if live(m):
                 times_cos(m, FIRST)
                 times_sin(m, FIRST, LOW)
-            if live(m - 1):
-                add_products(m - 1, SECOND, nc.vector)
-                store_rotated(m - 1)
-            if live(m + 2):
-                quantise(m + 2)
-            if m == -2:
-                negate_sin()
-            if live(m):
                 times_sin(m, FIRST, HIGH)
-                add_products(m, FIRST, nc.gpsimd)
+                if m == last:
+                    add_products(m, 0, 2, nc.gpsimd)
                 back_rotated(m, SECOND)
                 back_value_and_store(m)
+            if live(m + 1):
+                project(m + 1, (LOW, HIGH, VALUE))
             if live(m + 3):
                 transpose_x(m + 3, 0)
-            if live(m + 1):
-                project(m + 1, (VALUE,))
-                back_rotated(m + 1, FIRST)
-            if live(m + 3):
                 transpose_x(m + 3, 1)
             if m == -3:
                 bias_onto_partitions()
+            if live(m + 1):
+                back_rotated(m + 1, FIRST)
             if live(m):
                 times_cos(m, SECOND)
                 times_sin(m, SECOND, LOW)
                 times_sin(m, SECOND, HIGH)
+                if m == last:
+                    add_products(m, 2, 2, nc.vector)
+                else:
+                    add_products(m, 0, TILES, nc.gpsimd)
+                store_rotated(m)

@@ -47,12 +47,12 @@ def tile_causalselfattention_pa_t_kernel(
     with ExitStack() as ctx:
         ctx.enter_context(tc.manual_schedule())
         const = ctx.enter_context(tc.tile_pool(name="const", bufs=1))
-        x_pool = ctx.enter_context(tc.tile_pool(name="x", bufs=ROUNDS))
+        x_pool = ctx.enter_context(tc.tile_pool(name="x", bufs=BATCH))
         quant_pool = ctx.enter_context(tc.tile_pool(name="quant", bufs=2))
         grouped_pool = ctx.enter_context(tc.tile_pool(name="grouped", bufs=3))
         feat_pool = ctx.enter_context(tc.tile_pool(name="feat", bufs=2 * OPERANDS))
         prod_pool = ctx.enter_context(tc.tile_pool(name="prod", bufs=2))
-        out_pool = ctx.enter_context(tc.tile_pool(name="out", bufs=8))
+        out_pool = ctx.enter_context(tc.tile_pool(name="out", bufs=2))
         psum_xt = ctx.enter_context(tc.psum_pool(name="psum_xt", bufs=2))
         psum_acc = ctx.enter_context(tc.psum_pool(name="psum_acc", bufs=OPERANDS))
         psum_tok = ctx.enter_context(tc.psum_pool(name="psum_tok", bufs=1))
@@ -62,16 +62,18 @@ def tile_causalselfattention_pa_t_kernel(
             return b, slice(TILES * jq, TILES * (jq + 1))
 
         x_tiles = []
-
-        def load_x(r):
-            b, places = round_place(r)
-            x_sb = x_pool.tile([P, TILES, K], BF16)
-            rows = x[b].rearrange("(p j) k -> p j k", j=TOKENS_PER_PARTITION)[:, places, :]
-            for first in range(0, TILES, 2):
-                nc.sync.dma_start(out=x_sb[:, first : first + 2, :], in_=rows[:, first : first + 2, :])
+        for b in range(BATCH):
+            x_sb = x_pool.tile([P, TOKENS_PER_PARTITION, K], BF16, tag="x")
             x_tiles.append(x_sb)
 
-        load_x(0)
+        def load_x(b, first, count):
+            rows = x[b].rearrange("(p j) k -> p j k", j=TOKENS_PER_PARTITION)
+            nc.sync.dma_start(
+                out=x_tiles[b][:, first : first + count, :], in_=rows[:, first : first + count, :]
+            )
+
+        load_x(0, 0, 2)
+        load_x(0, 2, 2)
 
         w_words_in = const.tile([P, 2 * FEATURES], U8)
         nc.sync.dma_start(out=w_words_in[:].bitcast(I32), in_=qkv_w_words[0].bitcast(I32))
@@ -82,7 +84,7 @@ def tile_causalselfattention_pa_t_kernel(
                 out=w_scales_in[32 * quadrant : 32 * quadrant + 4, :].bitcast(I32),
                 in_=qkv_w_scales[0, 4 * quadrant : 4 * quadrant + 4, :].bitcast(I32),
             )
-        load_x(1)
+        load_x(0, TILES, TILES)
 
         bias_rows = const.tile([P, P], BF16)
         nc.vector.memset(bias_rows[:], 0.0)
@@ -102,8 +104,9 @@ def tile_causalselfattention_pa_t_kernel(
         nc.scalar.dma_start(
             out=sin_sb[:], in_=rope_sin[0, 0].rearrange("(p j) d -> p j d", j=TOKENS_PER_PARTITION)
         )
-        for r in range(2, ROUNDS):
-            load_x(r)
+        load_x(0, 2 * TILES, 2 * TILES)
+        for b in range(1, BATCH):
+            load_x(b, 0, TOKENS_PER_PARTITION)
 
         minus_sin_low = const.tile([P, TOKENS_PER_PARTITION, HALF], BF16)
 
@@ -147,7 +150,8 @@ def tile_causalselfattention_pa_t_kernel(
             if half_round == 0:
                 grouped_new = grouped_pool.tile([P, 4 * ROUND_TOKENS], BF16, align_bytes=64, tag="grouped")
                 grouped_tiles[r] = grouped_new
-            x_words = x_tiles[r][:].bitcast(F32)
+            b, places = round_place(r)
+            x_words = x_tiles[b][:].bitcast(F32)
             grouped_words = grouped_tiles[r][:].bitcast(F32)
             xt = psum_xt.tile([P, 2, 2 * P], F32, tag="xt")
             for tile_in_bank in range(2):
@@ -155,7 +159,7 @@ def tile_causalselfattention_pa_t_kernel(
                 for parity in range(2):
                     nc.tensor.transpose(
                         out=xt[:, parity, P * tile_in_bank : P * (tile_in_bank + 1)],
-                        in_=x_words[:, jj, parity:WORDS:2],
+                        in_=x_words[:, places.start + jj, parity:WORDS:2],
                         identity=identity[:],
                     )
             nc.scalar.copy(
@@ -250,25 +254,33 @@ def tile_causalselfattention_pa_t_kernel(
             )
 
         def add_products(r, first_tile, tiles, engine):
-            if first_tile == 0:
-                rotated_new = out_pool.tile([P, PAIRS, TILES, HEAD_DIM], F32, tag="rotated")
-                rotated_tiles[r] = rotated_new
+            b, places = round_place(r)
+            if places.start == 0 and first_tile == 0:
+                rotated_new = out_pool.tile([P, PAIRS, TOKENS_PER_PARTITION, HEAD_DIM], F32, tag="rotated")
+                rotated_tiles[b] = rotated_new
             chosen = slice(first_tile, first_tile + tiles)
+            target = slice(places.start + first_tile, places.start + first_tile + tiles)
             engine.tensor_tensor(
-                out=rotated_tiles[r][:, :, chosen, :].rearrange("p g j d -> p g (j d)"),
+                out=rotated_tiles[b][:, :, target, :].rearrange("p g j d -> p g (j d)"),
                 in0=prod_cos[r][:, :, chosen, :].rearrange("p g j d -> p g (j d)"),
                 in1=prod_sin[r][:, :, chosen, :].rearrange("p g j d -> p g (j d)"),
                 op=ALU.add,
             )
 
-        def place_in(out, r):
+        def store(out, tile_of_batch, r):
             b, places = round_place(r)
             rows = out[b].rearrange("h (p j) d -> p h j d", j=TOKENS_PER_PARTITION)
-            return rows[:, :, places, :]
+            if b == BATCH - 1:
+                nc.sync.dma_start(out=rows[:, :, places, :], in_=tile_of_batch[:, :, places, :])
+            elif places.stop == TOKENS_PER_PARTITION:
+                nc.sync.dma_start(out=rows, in_=tile_of_batch)
 
         def store_rotated(r):
-            nc.sync.dma_start(out=place_in(out_0, r), in_=rotated_tiles[r][:, 0:HEADS])
-            nc.sync.dma_start(out=place_in(out_1, r), in_=rotated_tiles[r][:, HEADS:PAIRS])
+            b, places = round_place(r)
+            store(out_0, rotated_tiles[b][:, 0:HEADS], r)
+            store(out_1, rotated_tiles[b][:, HEADS:PAIRS], r)
+
+        value_tiles = {}
 
         def back_value_and_store(r):
             tok = psum_tok.tile([P, TILES, P], F32, tag="tok_value")
@@ -278,13 +290,17 @@ def tile_causalselfattention_pa_t_kernel(
                     in_=features[(r, VALUE)][:, P * jj : P * (jj + 1)],
                     identity=identity[:],
                 )
-            value = out_pool.tile([P, HEADS, TILES, HEAD_DIM], F32, tag="value")
+            b, places = round_place(r)
+            if places.start == 0:
+                value_new = out_pool.tile([P, HEADS, TOKENS_PER_PARTITION, HEAD_DIM], F32, tag="value")
+                value_tiles[b] = value_new
+            value = value_tiles[b][:, :, places, :]
             for copy_out, tiles in ((nc.scalar.copy, slice(0, 2)), (nc.vector.tensor_copy, slice(2, 4))):
                 copy_out(
                     out=value[:, :, tiles, :].rearrange("p h j d -> p j h d"),
                     in_=tok[:, tiles, :].rearrange("p j (h d) -> p j h d", h=HEADS),
                 )
-            nc.sync.dma_start(out=place_in(out_2, r), in_=value[:])
+            store(out_2, value_tiles[b][:], r)
 
         def live(r):
             return 0 <= r < ROUNDS

@@ -88,14 +88,6 @@ def tile_causalselfattention_pa_t_kernel(
 
         bias_rows = const.tile([P, P], BF16)
         nc.vector.memset(bias_rows[:], 0.0)
-        nc.scalar.dma_start(
-            out=bias_rows[LOW : HIGH + 1, :].rearrange("f (g i) -> f g i", g=PAIRS),
-            in_=qkv_b[0 : 2 * P].rearrange("(g f i) -> f g i", g=PAIRS, f=2),
-        )
-        nc.scalar.dma_start(
-            out=bias_rows[VALUE : VALUE + 1, :],
-            in_=qkv_b[2 * P : 3 * P].rearrange("(o c) -> o c", o=1),
-        )
         cos_sb = const.tile([P, TOKENS_PER_PARTITION, HEAD_DIM], BF16)
         sin_sb = const.tile([P, TOKENS_PER_PARTITION, HEAD_DIM], BF16)
         nc.scalar.dma_start(
@@ -117,6 +109,14 @@ def tile_causalselfattention_pa_t_kernel(
 
         identity = const.tile([P, P], F32)
         make_identity(nc, identity[:])
+        nc.gpsimd.dma_start(
+            out=bias_rows[LOW : HIGH + 1, :].rearrange("f (g i) -> f g i", g=PAIRS),
+            in_=qkv_b[0 : 2 * P].rearrange("(g f i) -> f g i", g=PAIRS, f=2),
+        )
+        nc.gpsimd.dma_start(
+            out=bias_rows[VALUE : VALUE + 1, :],
+            in_=qkv_b[2 * P : 3 * P].rearrange("(o c) -> o c", o=1),
+        )
 
         w_words = const.tile([P, OPERANDS, 2 * P], U8, align_bytes=64)
         w_scales = const.tile([P, OPERANDS, P], U8, align_bytes=64)
@@ -134,10 +134,10 @@ def tile_causalselfattention_pa_t_kernel(
         )
 
         bias_rows_f32 = const.tile([P, P], F32)
-        nc.vector.tensor_copy(out=bias_rows_f32[:], in_=bias_rows[:])
         bias = const.tile([P, OPERANDS], F32)
 
         def bias_onto_partitions():
+            nc.vector.tensor_copy(out=bias_rows_f32[:], in_=bias_rows[:])
             bias_bank = psum_tok.tile([P, P], F32, tag="tok_value")
             nc.tensor.transpose(out=bias_bank[:], in_=bias_rows_f32[:], identity=identity[:])
             nc.vector.tensor_copy(out=bias[:], in_=bias_bank[:, 0:OPERANDS])
@@ -310,6 +310,7 @@ def tile_causalselfattention_pa_t_kernel(
             if live(m + 1):
                 quantise(m + 1)
             if m == -1:
+                bias_onto_partitions()
                 negate_sin()
             if live(m):
                 times_cos(m, FIRST)
@@ -324,8 +325,6 @@ def tile_causalselfattention_pa_t_kernel(
             if live(m + 3):
                 transpose_x(m + 3, 0)
                 transpose_x(m + 3, 1)
-            if m == -3:
-                bias_onto_partitions()
             if live(m + 1):
                 back_rotated(m + 1, FIRST)
             if live(m):

@@ -88,6 +88,7 @@ def tile_causalselfattention_pa_t_kernel(
 
         bias_rows = const.tile([P, P], BF16)
         nc.vector.memset(bias_rows[:], 0.0)
+        load_x(0, 2 * TILES, TILES)
         cos_sb = const.tile([P, TOKENS_PER_PARTITION, HEAD_DIM], BF16)
         sin_sb = const.tile([P, TOKENS_PER_PARTITION, HEAD_DIM], BF16)
         nc.scalar.dma_start(
@@ -96,7 +97,7 @@ def tile_causalselfattention_pa_t_kernel(
         nc.scalar.dma_start(
             out=sin_sb[:], in_=rope_sin[0, 0].rearrange("(p j) d -> p j d", j=TOKENS_PER_PARTITION)
         )
-        load_x(0, 2 * TILES, 2 * TILES)
+        load_x(0, 3 * TILES, TILES)
         for b in range(1, BATCH):
             load_x(b, 0, TOKENS_PER_PARTITION)
 

@@ -24,6 +24,7 @@ LOW, HIGH, VALUE = 0, 1, 2
 TOKENS_PER_PARTITION = SEQ // P
 TILES = 4
 ROUND_TOKENS = TILES * P
+TURNED = 3
 ROUNDS_PER_BATCH = TOKENS_PER_PARTITION // TILES
 ROUNDS = BATCH * ROUNDS_PER_BATCH
 WORDS = K // 2
@@ -48,7 +49,7 @@ def tile_causalselfattention_pa_t_kernel(
         ctx.enter_context(tc.manual_schedule())
         const = ctx.enter_context(tc.tile_pool(name="const", bufs=1))
         x_pool = ctx.enter_context(tc.tile_pool(name="x", bufs=BATCH))
-        quant_pool = ctx.enter_context(tc.tile_pool(name="quant", bufs=2))
+        quant_pool = ctx.enter_context(tc.tile_pool(name="quant", bufs=3))
         grouped_pool = ctx.enter_context(tc.tile_pool(name="grouped", bufs=3))
         feat_pool = ctx.enter_context(tc.tile_pool(name="feat", bufs=2 * OPERANDS))
         prod_pool = ctx.enter_context(tc.tile_pool(name="prod", bufs=2))
@@ -88,15 +89,15 @@ def tile_causalselfattention_pa_t_kernel(
 
         bias_rows = const.tile([P, P], BF16)
         nc.vector.memset(bias_rows[:], 0.0)
-        load_x(0, 2 * TILES, TILES)
         cos_sb = const.tile([P, TOKENS_PER_PARTITION, HEAD_DIM], BF16)
         sin_sb = const.tile([P, TOKENS_PER_PARTITION, HEAD_DIM], BF16)
-        nc.scalar.dma_start(
+        nc.sync.dma_start(
             out=cos_sb[:], in_=rope_cos[0, 0].rearrange("(p j) d -> p j d", j=TOKENS_PER_PARTITION)
         )
-        nc.scalar.dma_start(
+        nc.sync.dma_start(
             out=sin_sb[:], in_=rope_sin[0, 0].rearrange("(p j) d -> p j d", j=TOKENS_PER_PARTITION)
         )
+        load_x(0, 2 * TILES, TILES)
         load_x(0, 3 * TILES, TILES)
         for b in range(1, BATCH):
             load_x(b, 0, TOKENS_PER_PARTITION)
@@ -136,12 +137,22 @@ def tile_causalselfattention_pa_t_kernel(
 
         bias_rows_f32 = const.tile([P, P], F32)
         bias = const.tile([P, OPERANDS], F32)
+        value_bias = const.tile([P, P], F32)
 
         def bias_onto_partitions():
             nc.vector.tensor_copy(out=bias_rows_f32[:], in_=bias_rows[:])
             bias_bank = psum_tok.tile([P, P], F32, tag="tok_value")
             nc.tensor.transpose(out=bias_bank[:], in_=bias_rows_f32[:], identity=identity[:])
             nc.vector.tensor_copy(out=bias[:], in_=bias_bank[:, 0:OPERANDS])
+
+        def spread_value_bias():
+            value_bank = psum_tok.tile([P, P], F32, tag="tok_value")
+            nc.tensor.transpose(
+                out=value_bank[:],
+                in_=bias[:, VALUE : VALUE + 1].to_broadcast([P, P]),
+                identity=identity[:],
+            )
+            nc.vector.tensor_copy(out=value_bias[:], in_=value_bank[:])
 
         grouped_tiles = {}
         x_codes = {}
@@ -181,90 +192,82 @@ def tile_causalselfattention_pa_t_kernel(
 
         features = {}
 
+        def multiply_w(acc, r, s, first, tokens):
+            nc.tensor.matmul_mx(
+                out=acc[:, first : first + tokens],
+                lhsT=w_words[:, s, :].bitcast(FP4X4),
+                lhsT_scale=w_scales[:, s, :],
+                rhs=x_codes[r][:, first : first + tokens].bitcast(FP8X4),
+                rhs_scale=x_scales[r][:, first : first + tokens],
+                start=True,
+                stop=True,
+            )
+
         def project(r, operands):
             for s in operands:
                 acc = psum_acc.tile([P, ROUND_TOKENS], F32, tag="acc")
-                nc.tensor.matmul_mx(
-                    out=acc[:],
-                    lhsT=w_words[:, s, :].bitcast(FP4X4),
-                    lhsT_scale=w_scales[:, s, :],
-                    rhs=x_codes[r][:].bitcast(FP8X4),
-                    rhs_scale=x_scales[r][:],
-                    start=True,
-                    stop=True,
-                )
+                if s == VALUE:
+                    multiply_w(acc, r, s, 0, 2 * P)
+                    multiply_w(acc, r, s, 2 * P, P)
+                else:
+                    multiply_w(acc, r, s, 0, ROUND_TOKENS)
+                tokens = TURNED * P if s == VALUE else ROUND_TOKENS
                 feat = feat_pool.tile([P, ROUND_TOKENS], F32, tag="feat")
                 nc.scalar.activation(
-                    out=feat[:], in_=acc[:], func=ACT.Identity, bias=bias[:, s : s + 1], scale=1.0
+                    out=feat[:, 0:tokens],
+                    in_=acc[:, 0:tokens],
+                    func=ACT.Identity,
+                    bias=bias[:, s : s + 1],
+                    scale=1.0,
                 )
                 features[(r, s)] = feat
 
-        FIRST, SECOND = 0, 1
         banks = {}
         prod_cos = {}
         prod_sin = {}
         rotated_tiles = {}
 
-        def back_rotated(r, part):
-            tok = psum_tok.tile([P, 2, 2, P], F32, tag="tok_first" if part == FIRST else "tok_second")
-            for j in range(2):
-                jj = 2 * part + j
-                for s in (LOW, HIGH):
-                    nc.tensor.transpose(
-                        out=tok[:, j, s, :],
-                        in_=features[(r, s)][:, P * jj : P * (jj + 1)],
-                        identity=identity[:],
-                    )
-            banks[(r, part)] = tok
+        def back_rotated(r, s):
+            tok = psum_tok.tile([P, TILES, P], F32, tag="tok_low" if s == LOW else "tok_high")
+            for jj in range(TILES):
+                nc.tensor.transpose(
+                    out=tok[:, jj, :],
+                    in_=features[(r, s)][:, P * jj : P * (jj + 1)],
+                    identity=identity[:],
+                )
+            banks[(r, s)] = tok
 
-        def part_places(r, part):
-            b, jq = divmod(r, ROUNDS_PER_BATCH)
-            first = TILES * jq + 2 * part
-            return slice(first, first + 2)
+        def multiply(r, s, table, product, half):
+            nc.vector.tensor_tensor(
+                out=product[:, :, :, HALF * half : HALF * (half + 1)].rearrange("p g j i -> p j g i"),
+                in0=banks[(r, s)][:].rearrange("p j (g i) -> p j g i", g=PAIRS),
+                in1=table.unsqueeze(2).to_broadcast([P, TILES, PAIRS, HALF]),
+                op=ALU.mult,
+            )
 
-        def times_cos(r, part):
-            places = part_places(r, part)
-            if part == FIRST:
+        def rotate_products(r, s):
+            b, places = round_place(r)
+            if s == LOW:
                 prod_new = prod_pool.tile([P, PAIRS, TILES, HEAD_DIM], F32, tag="prod_cos")
                 prod_cos[r] = prod_new
-            table = cos_sb[:, places, :].rearrange("p j (f i) -> p (j f) i", f=2)
-            nc.vector.tensor_tensor(
-                out=prod_cos[r][:, :, 2 * part : 2 * part + 2, :].rearrange("p g j (f i) -> p (j f) g i", f=2),
-                in0=banks[(r, part)][:].rearrange("p j f (g i) -> p (j f) g i", g=PAIRS),
-                in1=table.unsqueeze(2).to_broadcast([P, 4, PAIRS, HALF]),
-                op=ALU.mult,
-            )
-
-        def times_sin(r, part, source):
-            places = part_places(r, part)
-            if source == LOW and part == FIRST:
                 prod_new = prod_pool.tile([P, PAIRS, TILES, HEAD_DIM], F32, tag="prod_sin")
                 prod_sin[r] = prod_new
-            tiles = slice(2 * part, 2 * part + 2)
-            if source == LOW:
-                table = sin_sb[:, places, HALF:HEAD_DIM]
-                target = prod_sin[r][:, :, tiles, HALF:HEAD_DIM]
+                multiply(r, LOW, cos_sb[:, places, 0:HALF], prod_cos[r], 0)
+                multiply(r, LOW, sin_sb[:, places, HALF:HEAD_DIM], prod_sin[r], 1)
             else:
-                table = minus_sin_low[:, places, :]
-                target = prod_sin[r][:, :, tiles, 0:HALF]
-            nc.vector.tensor_tensor(
-                out=target.rearrange("p g j i -> p j g i"),
-                in0=banks[(r, part)][:, :, source, :].rearrange("p j (g i) -> p j g i", g=PAIRS),
-                in1=table.unsqueeze(2).to_broadcast([P, 2, PAIRS, HALF]),
-                op=ALU.mult,
-            )
+                multiply(r, HIGH, cos_sb[:, places, HALF:HEAD_DIM], prod_cos[r], 1)
+                add_value_bias_and_store(r)
+                multiply(r, HIGH, minus_sin_low[:, places, :], prod_sin[r], 0)
 
-        def add_products(r, first_tile, tiles, engine):
+        def add_products(r, pairs, engine):
             b, places = round_place(r)
-            if places.start == 0 and first_tile == 0:
+            if places.start == 0 and b not in rotated_tiles:
                 rotated_new = out_pool.tile([P, PAIRS, TOKENS_PER_PARTITION, HEAD_DIM], F32, tag="rotated")
                 rotated_tiles[b] = rotated_new
-            chosen = slice(first_tile, first_tile + tiles)
-            target = slice(places.start + first_tile, places.start + first_tile + tiles)
             engine.tensor_tensor(
-                out=rotated_tiles[b][:, :, target, :].rearrange("p g j d -> p g (j d)"),
-                in0=prod_cos[r][:, :, chosen, :].rearrange("p g j d -> p g (j d)"),
-                in1=prod_sin[r][:, :, chosen, :].rearrange("p g j d -> p g (j d)"),
+                out=rotated_tiles[b][:, pairs, places, :].rearrange("p g j d -> p g (j d)"),
+                in0=prod_cos[r][:, pairs].rearrange("p g j d -> p g (j d)"),
+                in1=prod_sin[r][:, pairs].rearrange("p g j d -> p g (j d)"),
                 op=ALU.add,
             )
 
@@ -276,31 +279,54 @@ def tile_causalselfattention_pa_t_kernel(
             elif places.stop == TOKENS_PER_PARTITION:
                 nc.sync.dma_start(out=rows, in_=tile_of_batch)
 
-        def store_rotated(r):
+        QUERY, KEY, BOTH = slice(0, HEADS), slice(HEADS, PAIRS), slice(0, PAIRS)
+
+        def store_rotated(r, out, pairs):
             b, places = round_place(r)
-            store(out_0, rotated_tiles[b][:, 0:HEADS], r)
-            store(out_1, rotated_tiles[b][:, HEADS:PAIRS], r)
+            store(out, rotated_tiles[b][:, pairs], r)
 
         value_tiles = {}
 
-        def back_value_and_store(r):
+        def back_value(r):
             tok = psum_tok.tile([P, TILES, P], F32, tag="tok_value")
-            for jj in range(TILES):
+            for jj in range(TURNED):
                 nc.tensor.transpose(
                     out=tok[:, jj, :],
                     in_=features[(r, VALUE)][:, P * jj : P * (jj + 1)],
                     identity=identity[:],
+                )
+            for jj in range(TURNED, TILES):
+                nc.tensor.matmul_mx(
+                    out=tok[:, jj, :],
+                    lhsT=x_codes[r][:, P * jj : P * (jj + 1)].bitcast(FP8X4),
+                    lhsT_scale=x_scales[r][:, P * jj : P * (jj + 1)],
+                    rhs=w_words[:, VALUE, :].bitcast(FP4X4),
+                    rhs_scale=w_scales[:, VALUE, :],
+                    start=True,
+                    stop=True,
                 )
             b, places = round_place(r)
             if places.start == 0:
                 value_new = out_pool.tile([P, HEADS, TOKENS_PER_PARTITION, HEAD_DIM], F32, tag="value")
                 value_tiles[b] = value_new
             value = value_tiles[b][:, :, places, :]
-            for copy_out, tiles in ((nc.scalar.copy, slice(0, 2)), (nc.vector.tensor_copy, slice(2, 4))):
-                copy_out(
-                    out=value[:, :, tiles, :].rearrange("p h j d -> p j h d"),
-                    in_=tok[:, tiles, :].rearrange("p j (h d) -> p j h d", h=HEADS),
-                )
+            nc.scalar.copy(
+                out=value[:, :, 0:TURNED, :].rearrange("p h j d -> p j h d"),
+                in_=tok[:, 0:TURNED, :].rearrange("p j (h d) -> p j h d", h=HEADS),
+            )
+            banks[(r, VALUE)] = tok
+
+        def add_value_bias_and_store(r):
+            b, places = round_place(r)
+            nc.vector.tensor_tensor(
+                out=value_tiles[b][:, :, places.start + TURNED : places.stop, :].rearrange("p h j d -> p j h d"),
+                in0=banks[(r, VALUE)][:, TURNED:TILES, :].rearrange("p j (h d) -> p j h d", h=HEADS),
+                in1=value_bias[:]
+                .rearrange("p (h d) -> p h d", h=HEADS)
+                .unsqueeze(1)
+                .to_broadcast([P, TILES - TURNED, HEADS, HEAD_DIM]),
+                op=ALU.add,
+            )
             store(out_2, value_tiles[b][:], r)
 
         def live(r):
@@ -311,29 +337,28 @@ def tile_causalselfattention_pa_t_kernel(
             if live(m + 1):
                 quantise(m + 1)
             if m == -1:
-                bias_onto_partitions()
                 negate_sin()
+                spread_value_bias()
             if live(m):
-                times_cos(m, FIRST)
-                times_sin(m, FIRST, LOW)
-                times_sin(m, FIRST, HIGH)
-                if m == last:
-                    add_products(m, 0, 2, nc.gpsimd)
-                back_rotated(m, SECOND)
-                back_value_and_store(m)
+                rotate_products(m, LOW)
+                back_rotated(m, HIGH)
+                back_value(m)
             if live(m + 1):
                 project(m + 1, (LOW, HIGH, VALUE))
             if live(m + 3):
                 transpose_x(m + 3, 0)
+                if m == -2:
+                    bias_onto_partitions()
                 transpose_x(m + 3, 1)
             if live(m + 1):
-                back_rotated(m + 1, FIRST)
+                back_rotated(m + 1, LOW)
             if live(m):
-                times_cos(m, SECOND)
-                times_sin(m, SECOND, LOW)
-                times_sin(m, SECOND, HIGH)
+                rotate_products(m, HIGH)
                 if m == last:
-                    add_products(m, 2, 2, nc.vector)
+                    for out, pairs in ((out_0, QUERY), (out_1, KEY)):
+                        add_products(m, pairs, nc.vector)
+                        store_rotated(m, out, pairs)
                 else:
-                    add_products(m, 0, TILES, nc.gpsimd)
-                store_rotated(m)
+                    add_products(m, BOTH, nc.gpsimd)
+                    store_rotated(m, out_0, QUERY)
+                    store_rotated(m, out_1, KEY)

@@ -17,10 +17,9 @@ P = 128
 BATCH, SEQ, K = 4, 2048, 512
 HEADS, HEAD_DIM = 2, 64
 HALF = HEAD_DIM // 2
-PAIRS = 2 * HEADS
 FEATURES = 3 * HEADS * HEAD_DIM
-OPERANDS = FEATURES // P
-LOW, HIGH, VALUE = 0, 1, 2
+STREAMS = FEATURES // P
+QUERY, KEY, VALUE = 0, 1, 2
 TOKENS_PER_PARTITION = SEQ // P
 TILES = 4
 ROUND_TOKENS = TILES * P
@@ -30,15 +29,6 @@ ROUNDS = BATCH * ROUNDS_PER_BATCH
 WORDS = K // 2
 
 FLOPS = 2 * BATCH * SEQ * K * FEATURES
-
-
-def regroup_columns(nc, dst, src, width):
-    rotated = 2 * PAIRS * width
-    nc.vector.tensor_copy(
-        out=dst[:, 0:rotated].rearrange("p (f g i) -> p f g i", f=2, g=PAIRS),
-        in_=src[:, 0:rotated].rearrange("p (g f i) -> p f g i", g=PAIRS, f=2),
-    )
-    nc.vector.tensor_copy(out=dst[:, rotated:], in_=src[:, rotated:])
 
 
 def tile_causalselfattention_pa_t_kernel(
@@ -51,11 +41,11 @@ def tile_causalselfattention_pa_t_kernel(
         x_pool = ctx.enter_context(tc.tile_pool(name="x", bufs=BATCH))
         quant_pool = ctx.enter_context(tc.tile_pool(name="quant", bufs=3))
         grouped_pool = ctx.enter_context(tc.tile_pool(name="grouped", bufs=3))
-        feat_pool = ctx.enter_context(tc.tile_pool(name="feat", bufs=2 * OPERANDS))
+        feat_pool = ctx.enter_context(tc.tile_pool(name="feat", bufs=2 * STREAMS))
         prod_pool = ctx.enter_context(tc.tile_pool(name="prod", bufs=2))
         out_pool = ctx.enter_context(tc.tile_pool(name="out", bufs=2))
         psum_xt = ctx.enter_context(tc.psum_pool(name="psum_xt", bufs=2))
-        psum_acc = ctx.enter_context(tc.psum_pool(name="psum_acc", bufs=OPERANDS))
+        psum_acc = ctx.enter_context(tc.psum_pool(name="psum_acc", bufs=STREAMS))
         psum_tok = ctx.enter_context(tc.psum_pool(name="psum_tok", bufs=1))
 
         def round_place(r):
@@ -73,22 +63,25 @@ def tile_causalselfattention_pa_t_kernel(
                 out=x_tiles[b][:, first : first + count, :], in_=rows[:, first : first + count, :]
             )
 
+        bias_rows = const.tile([P, P], BF16)
+        nc.vector.memset(bias_rows[:], 0.0)
         load_x(0, 0, 2)
         load_x(0, 2, 2)
 
-        w_words_in = const.tile([P, 2 * FEATURES], U8)
-        nc.sync.dma_start(out=w_words_in[:].bitcast(I32), in_=qkv_w_words[0].bitcast(I32))
-        w_scales_in = const.tile([P, FEATURES], U8)
-        nc.vector.memset(w_scales_in[:].bitcast(I32), 0)
+        w_words = const.tile([P, STREAMS, 2 * P], U8, align_bytes=64)
+        nc.sync.dma_start(
+            out=w_words[:].rearrange("p s c -> p (s c)").bitcast(I32), in_=qkv_w_words[0].bitcast(I32)
+        )
+        w_scales = const.tile([P, STREAMS, P], U8, align_bytes=64)
+        scale_words = w_scales[:].rearrange("p s c -> p (s c)").bitcast(I32)
+        nc.vector.memset(scale_words, 0)
         for quadrant in range(4):
             nc.sync.dma_start(
-                out=w_scales_in[32 * quadrant : 32 * quadrant + 4, :].bitcast(I32),
+                out=scale_words[32 * quadrant : 32 * quadrant + 4, :],
                 in_=qkv_w_scales[0, 4 * quadrant : 4 * quadrant + 4, :].bitcast(I32),
             )
         load_x(0, TILES, TILES)
 
-        bias_rows = const.tile([P, P], BF16)
-        nc.vector.memset(bias_rows[:], 0.0)
         cos_sb = const.tile([P, TOKENS_PER_PARTITION, HEAD_DIM], BF16)
         sin_sb = const.tile([P, TOKENS_PER_PARTITION, HEAD_DIM], BF16)
         nc.sync.dma_start(
@@ -102,48 +95,24 @@ def tile_causalselfattention_pa_t_kernel(
         for b in range(1, BATCH):
             load_x(b, 0, TOKENS_PER_PARTITION)
 
-        minus_sin_low = const.tile([P, TOKENS_PER_PARTITION, HALF], BF16)
-
         def negate_sin():
             nc.vector.tensor_scalar(
-                out=minus_sin_low[:], in0=sin_sb[:, :, 0:HALF], scalar1=-1.0, scalar2=None, op0=ALU.mult
+                out=sin_sb[:, :, 0:HALF], in0=sin_sb[:, :, 0:HALF], scalar1=-1.0, scalar2=None, op0=ALU.mult
             )
 
         identity = const.tile([P, P], F32)
         make_identity(nc, identity[:])
-        nc.gpsimd.dma_start(
-            out=bias_rows[LOW : HIGH + 1, :].rearrange("f (g i) -> f g i", g=PAIRS),
-            in_=qkv_b[0 : 2 * P].rearrange("(g f i) -> f g i", g=PAIRS, f=2),
-        )
-        nc.gpsimd.dma_start(
-            out=bias_rows[VALUE : VALUE + 1, :],
-            in_=qkv_b[2 * P : 3 * P].rearrange("(o c) -> o c", o=1),
-        )
-
-        w_words = const.tile([P, OPERANDS, 2 * P], U8, align_bytes=64)
-        w_scales = const.tile([P, OPERANDS, P], U8, align_bytes=64)
-        regroup_columns(
-            nc,
-            w_words[:].rearrange("p s c -> p (s c)").bitcast(I32),
-            w_words_in[:].bitcast(I32),
-            2 * HALF // 4,
-        )
-        regroup_columns(
-            nc,
-            w_scales[:].rearrange("p s c -> p (s c)").bitcast(I32),
-            w_scales_in[:].bitcast(I32),
-            HALF // 4,
-        )
+        nc.gpsimd.dma_start(out=bias_rows[0:STREAMS, :], in_=qkv_b.rearrange("(o c) -> o c", o=STREAMS))
 
         bias_rows_f32 = const.tile([P, P], F32)
-        bias = const.tile([P, OPERANDS], F32)
+        bias = const.tile([P, STREAMS], F32)
         value_bias = const.tile([P, P], F32)
 
         def bias_onto_partitions():
             nc.vector.tensor_copy(out=bias_rows_f32[:], in_=bias_rows[:])
             bias_bank = psum_tok.tile([P, P], F32, tag="tok_value")
             nc.tensor.transpose(out=bias_bank[:], in_=bias_rows_f32[:], identity=identity[:])
-            nc.vector.tensor_copy(out=bias[:], in_=bias_bank[:, 0:OPERANDS])
+            nc.vector.tensor_copy(out=bias[:], in_=bias_bank[:, 0:STREAMS])
 
         def spread_value_bias():
             value_bank = psum_tok.tile([P, P], F32, tag="tok_value")
@@ -228,7 +197,7 @@ def tile_causalselfattention_pa_t_kernel(
         rotated_tiles = {}
 
         def back_rotated(r, s):
-            tok = psum_tok.tile([P, TILES, P], F32, tag="tok_low" if s == LOW else "tok_high")
+            tok = psum_tok.tile([P, TILES, P], F32, tag="tok_query" if s == QUERY else "tok_key")
             for jj in range(TILES):
                 nc.tensor.transpose(
                     out=tok[:, jj, :],
@@ -237,37 +206,42 @@ def tile_causalselfattention_pa_t_kernel(
                 )
             banks[(r, s)] = tok
 
-        def multiply(r, s, table, product, half):
+        def product_tile(r, s, products, tag):
+            if s == QUERY:
+                prod_new = prod_pool.tile([P, 2 * HEADS, TILES, HEAD_DIM], F32, tag=tag)
+                products[r] = prod_new
+            return products[r][:, HEADS * s : HEADS * (s + 1)]
+
+        def times_cos(r, s):
+            b, places = round_place(r)
             nc.vector.tensor_tensor(
-                out=product[:, :, :, HALF * half : HALF * (half + 1)].rearrange("p g j i -> p j g i"),
-                in0=banks[(r, s)][:].rearrange("p j (g i) -> p j g i", g=PAIRS),
-                in1=table.unsqueeze(2).to_broadcast([P, TILES, PAIRS, HALF]),
+                out=product_tile(r, s, prod_cos, "prod_cos").rearrange("p h j d -> p j h d"),
+                in0=banks[(r, s)][:].rearrange("p j (h d) -> p j h d", h=HEADS),
+                in1=cos_sb[:, places, :].unsqueeze(2).to_broadcast([P, TILES, HEADS, HEAD_DIM]),
                 op=ALU.mult,
             )
 
-        def rotate_products(r, s):
+        def times_sin(r, s):
             b, places = round_place(r)
-            if s == LOW:
-                prod_new = prod_pool.tile([P, PAIRS, TILES, HEAD_DIM], F32, tag="prod_cos")
-                prod_cos[r] = prod_new
-                prod_new = prod_pool.tile([P, PAIRS, TILES, HEAD_DIM], F32, tag="prod_sin")
-                prod_sin[r] = prod_new
-                multiply(r, LOW, cos_sb[:, places, 0:HALF], prod_cos[r], 0)
-                multiply(r, LOW, sin_sb[:, places, HALF:HEAD_DIM], prod_sin[r], 1)
-            else:
-                multiply(r, HIGH, cos_sb[:, places, HALF:HEAD_DIM], prod_cos[r], 1)
-                add_value_bias_and_store(r)
-                multiply(r, HIGH, minus_sin_low[:, places, :], prod_sin[r], 0)
+            halves = banks[(r, s)][:].rearrange("p j (h f i) -> p j h f i", h=HEADS, f=2)
+            table = sin_sb[:, places, :].rearrange("p j (f i) -> p j f i", f=2)
+            nc.vector.tensor_tensor(
+                out=product_tile(r, s, prod_sin, "prod_sin").rearrange("p h j (f i) -> p j h f i", f=2),
+                in0=halves[:, :, :, ::-1, :],
+                in1=table.unsqueeze(2).to_broadcast([P, TILES, HEADS, 2, HALF]),
+                op=ALU.mult,
+            )
 
-        def add_products(r, pairs, engine):
+        def add_products(r, streams, engine):
             b, places = round_place(r)
             if places.start == 0 and b not in rotated_tiles:
-                rotated_new = out_pool.tile([P, PAIRS, TOKENS_PER_PARTITION, HEAD_DIM], F32, tag="rotated")
+                rotated_new = out_pool.tile([P, 2 * HEADS, TOKENS_PER_PARTITION, HEAD_DIM], F32, tag="rotated")
                 rotated_tiles[b] = rotated_new
+            heads = slice(HEADS * streams.start, HEADS * streams.stop)
             engine.tensor_tensor(
-                out=rotated_tiles[b][:, pairs, places, :].rearrange("p g j d -> p g (j d)"),
-                in0=prod_cos[r][:, pairs].rearrange("p g j d -> p g (j d)"),
-                in1=prod_sin[r][:, pairs].rearrange("p g j d -> p g (j d)"),
+                out=rotated_tiles[b][:, heads, places, :].rearrange("p g j d -> p g (j d)"),
+                in0=prod_cos[r][:, heads].rearrange("p g j d -> p g (j d)"),
+                in1=prod_sin[r][:, heads].rearrange("p g j d -> p g (j d)"),
                 op=ALU.add,
             )
 
@@ -279,11 +253,9 @@ def tile_causalselfattention_pa_t_kernel(
             elif places.stop == TOKENS_PER_PARTITION:
                 nc.sync.dma_start(out=rows, in_=tile_of_batch)
 
-        QUERY, KEY, BOTH = slice(0, HEADS), slice(HEADS, PAIRS), slice(0, PAIRS)
-
-        def store_rotated(r, out, pairs):
+        def store_rotated(r, out, s):
             b, places = round_place(r)
-            store(out, rotated_tiles[b][:, pairs], r)
+            store(out, rotated_tiles[b][:, HEADS * s : HEADS * (s + 1)], r)
 
         value_tiles = {}
 
@@ -337,28 +309,31 @@ def tile_causalselfattention_pa_t_kernel(
             if live(m + 1):
                 quantise(m + 1)
             if m == -1:
+                bias_onto_partitions()
                 negate_sin()
                 spread_value_bias()
             if live(m):
-                rotate_products(m, LOW)
-                back_rotated(m, HIGH)
+                times_cos(m, QUERY)
+                times_sin(m, QUERY)
+                if m == last:
+                    add_products(m, slice(QUERY, KEY), nc.gpsimd)
+                    store_rotated(m, out_0, QUERY)
+                back_rotated(m, KEY)
                 back_value(m)
             if live(m + 1):
-                project(m + 1, (LOW, HIGH, VALUE))
+                project(m + 1, (QUERY, KEY, VALUE))
             if live(m + 3):
                 transpose_x(m + 3, 0)
-                if m == -2:
-                    bias_onto_partitions()
                 transpose_x(m + 3, 1)
             if live(m + 1):
-                back_rotated(m + 1, LOW)
+                back_rotated(m + 1, QUERY)
             if live(m):
-                rotate_products(m, HIGH)
+                times_cos(m, KEY)
+                add_value_bias_and_store(m)
+                times_sin(m, KEY)
                 if m == last:
-                    for out, pairs in ((out_0, QUERY), (out_1, KEY)):
-                        add_products(m, pairs, nc.vector)
-                        store_rotated(m, out, pairs)
+                    add_products(m, slice(KEY, VALUE), nc.vector)
                 else:
-                    add_products(m, BOTH, nc.gpsimd)
+                    add_products(m, slice(QUERY, VALUE), nc.gpsimd)
                     store_rotated(m, out_0, QUERY)
-                    store_rotated(m, out_1, KEY)
+                store_rotated(m, out_1, KEY)

@@ -104,24 +104,30 @@ def tile_causalselfattention_pa_t_kernel(
         make_identity(nc, identity[:])
         nc.gpsimd.dma_start(out=bias_rows[0:STREAMS, :], in_=qkv_b.rearrange("(o c) -> o c", o=STREAMS))
 
+        banks = {}
         bias_rows_f32 = const.tile([P, P], F32)
         bias = const.tile([P, STREAMS], F32)
         value_bias = const.tile([P, P], F32)
 
-        def bias_onto_partitions():
+        def widen_bias():
             nc.vector.tensor_copy(out=bias_rows_f32[:], in_=bias_rows[:])
+
+        def bias_onto_partitions():
             bias_bank = psum_tok.tile([P, P], F32, tag="tok_value")
             nc.tensor.transpose(out=bias_bank[:], in_=bias_rows_f32[:], identity=identity[:])
             nc.vector.tensor_copy(out=bias[:], in_=bias_bank[:, 0:STREAMS])
 
-        def spread_value_bias():
+        def turn_value_bias():
             value_bank = psum_tok.tile([P, P], F32, tag="tok_value")
+            banks["bias"] = value_bank
             nc.tensor.transpose(
                 out=value_bank[:],
                 in_=bias[:, VALUE : VALUE + 1].to_broadcast([P, P]),
                 identity=identity[:],
             )
-            nc.vector.tensor_copy(out=value_bias[:], in_=value_bank[:])
+
+        def copy_value_bias():
+            nc.vector.tensor_copy(out=value_bias[:], in_=banks["bias"][:])
 
         grouped_tiles = {}
         x_codes = {}
@@ -191,7 +197,6 @@ def tile_causalselfattention_pa_t_kernel(
                 )
                 features[(r, s)] = feat
 
-        banks = {}
         prod_cos = {}
         prod_sin = {}
         rotated_tiles = {}
@@ -250,8 +255,9 @@ def tile_causalselfattention_pa_t_kernel(
             rows = out[b].rearrange("h (p j) d -> p h j d", j=TOKENS_PER_PARTITION)
             if b == BATCH - 1:
                 nc.sync.dma_start(out=rows[:, :, places, :], in_=tile_of_batch[:, :, places, :])
-            elif places.stop == TOKENS_PER_PARTITION:
-                nc.sync.dma_start(out=rows, in_=tile_of_batch)
+            elif places.stop % 8 == 0:
+                places = slice(places.stop - 8, places.stop)
+                nc.sync.dma_start(out=rows[:, :, places, :], in_=tile_of_batch[:, :, places, :])
 
         def store_rotated(r, out, s):
             b, places = round_place(r)
@@ -311,17 +317,19 @@ def tile_causalselfattention_pa_t_kernel(
             if m == -1:
                 bias_onto_partitions()
                 negate_sin()
-                spread_value_bias()
+            if m == 0:
+                copy_value_bias()
             if live(m):
                 times_cos(m, QUERY)
                 times_sin(m, QUERY)
-                if m == last:
-                    add_products(m, slice(QUERY, KEY), nc.gpsimd)
-                    store_rotated(m, out_0, QUERY)
                 back_rotated(m, KEY)
                 back_value(m)
             if live(m + 1):
                 project(m + 1, (QUERY, KEY, VALUE))
+            if m == -1:
+                turn_value_bias()
+            if m == -2:
+                widen_bias()
             if live(m + 3):
                 transpose_x(m + 3, 0)
                 transpose_x(m + 3, 1)
@@ -332,6 +340,8 @@ def tile_causalselfattention_pa_t_kernel(
                 add_value_bias_and_store(m)
                 times_sin(m, KEY)
                 if m == last:
+                    add_products(m, slice(QUERY, KEY), nc.vector)
+                    store_rotated(m, out_0, QUERY)
                     add_products(m, slice(KEY, VALUE), nc.vector)
                 else:
                     add_products(m, slice(QUERY, VALUE), nc.gpsimd)

@@ -27,6 +27,7 @@ TURNED = 3
 ROUNDS_PER_BATCH = TOKENS_PER_PARTITION // TILES
 ROUNDS = BATCH * ROUNDS_PER_BATCH
 WORDS = K // 2
+WARM_UPS = 4
 
 FLOPS = 2 * BATCH * SEQ * K * FEATURES
 
@@ -62,6 +63,12 @@ def tile_causalselfattention_pa_t_kernel(
             nc.sync.dma_start(
                 out=x_tiles[b][:, first : first + count, :], in_=rows[:, first : first + count, :]
             )
+
+        zeros = const.tile([P, ROUND_TOKENS], BF16)
+        nc.vector.memset(zeros[:], 0.0)
+        unread = psum_tok.tile([P, ROUND_TOKENS], F32, tag="tok_value")
+        for repeat in range(WARM_UPS):
+            nc.tensor.matmul(out=unread[:], lhsT=zeros[:, 0:P], rhs=zeros[:], start=True, stop=True)
 
         bias_rows = const.tile([P, P], BF16)
         nc.vector.memset(bias_rows[:], 0.0)
@@ -149,7 +156,8 @@ def tile_causalselfattention_pa_t_kernel(
                         in_=x_words[:, places.start + jj, parity:WORDS:2],
                         identity=identity[:],
                     )
-            nc.scalar.copy(
+            copy_out = nc.vector.tensor_copy if (r, half_round) == (0, 1) else nc.scalar.copy
+            copy_out(
                 out=grouped_words[:, 4 * P * half_round : 4 * P * (half_round + 1)].rearrange(
                     "p (n u) -> p n u", u=2
                 ),

@@ -64,11 +64,21 @@ def tile_causalselfattention_pa_t_kernel(
                 out=x_tiles[b][:, first : first + count, :], in_=rows[:, first : first + count, :]
             )
 
-        zeros = const.tile([P, ROUND_TOKENS], BF16)
+        w_scales = const.tile([P, STREAMS, P], U8, align_bytes=64)
+        scale_words = w_scales[:].rearrange("p s c -> p (s c)").bitcast(I32)
+        nc.vector.memset(scale_words, 0)
+
+        zeros = const.tile([P, P], BF16)
         nc.vector.memset(zeros[:], 0.0)
-        unread = psum_tok.tile([P, ROUND_TOKENS], F32, tag="tok_value")
+        unread = psum_tok.tile([P, TILES, P], F32, tag="tok_value")
         for repeat in range(WARM_UPS):
-            nc.tensor.matmul(out=unread[:], lhsT=zeros[:, 0:P], rhs=zeros[:], start=True, stop=True)
+            nc.tensor.matmul(
+                out=unread[:],
+                lhsT=zeros[:],
+                rhs=zeros[:].unsqueeze(1).to_broadcast([P, TILES, P]),
+                start=True,
+                stop=True,
+            )
 
         bias_rows = const.tile([P, P], BF16)
         nc.vector.memset(bias_rows[:], 0.0)
@@ -79,9 +89,6 @@ def tile_causalselfattention_pa_t_kernel(
         nc.sync.dma_start(
             out=w_words[:].rearrange("p s c -> p (s c)").bitcast(I32), in_=qkv_w_words[0].bitcast(I32)
         )
-        w_scales = const.tile([P, STREAMS, P], U8, align_bytes=64)
-        scale_words = w_scales[:].rearrange("p s c -> p (s c)").bitcast(I32)
-        nc.vector.memset(scale_words, 0)
         for quadrant in range(4):
             nc.sync.dma_start(
                 out=scale_words[32 * quadrant : 32 * quadrant + 4, :],
@@ -245,16 +252,15 @@ def tile_causalselfattention_pa_t_kernel(
                 op=ALU.mult,
             )
 
-        def add_products(r, streams, engine):
+        def add_products(r, pairs, engine):
             b, places = round_place(r)
             if places.start == 0 and b not in rotated_tiles:
                 rotated_new = out_pool.tile([P, 2 * HEADS, TOKENS_PER_PARTITION, HEAD_DIM], F32, tag="rotated")
                 rotated_tiles[b] = rotated_new
-            heads = slice(HEADS * streams.start, HEADS * streams.stop)
             engine.tensor_tensor(
-                out=rotated_tiles[b][:, heads, places, :].rearrange("p g j d -> p g (j d)"),
-                in0=prod_cos[r][:, heads].rearrange("p g j d -> p g (j d)"),
-                in1=prod_sin[r][:, heads].rearrange("p g j d -> p g (j d)"),
+                out=rotated_tiles[b][:, pairs, places, :].rearrange("p g j d -> p g (j d)"),
+                in0=prod_cos[r][:, pairs].rearrange("p g j d -> p g (j d)"),
+                in1=prod_sin[r][:, pairs].rearrange("p g j d -> p g (j d)"),
                 op=ALU.add,
             )
 
@@ -346,12 +352,22 @@ def tile_causalselfattention_pa_t_kernel(
             if live(m):
                 times_cos(m, KEY)
                 add_value_bias_and_store(m)
+                if m == last:
+                    store_rotated(m - 1, out_1, KEY)
+                elif live(m - 1):
+                    store_rotated(m - 1, out_0, QUERY)
+                    store_rotated(m - 1, out_1, KEY)
                 times_sin(m, KEY)
                 if m == last:
-                    add_products(m, slice(QUERY, KEY), nc.vector)
+                    b, places = round_place(m)
+                    for pair in range(2 * HEADS):
+                        s, h = divmod(pair, HEADS)
+                        add_products(m, slice(pair, pair + 1), nc.vector)
+                        rows = (out_0, out_1)[s][b, h].rearrange("(p j) d -> p j d", j=TOKENS_PER_PARTITION)
+                        nc.sync.dma_start(out=rows[:, places, :], in_=rotated_tiles[b][:, pair, places, :])
+                elif m == last - 1:
+                    add_products(m, slice(0, HEADS), nc.gpsimd)
                     store_rotated(m, out_0, QUERY)
-                    add_products(m, slice(KEY, VALUE), nc.vector)
+                    add_products(m, slice(HEADS, 2 * HEADS), nc.gpsimd)
                 else:
-                    add_products(m, slice(QUERY, VALUE), nc.gpsimd)
-                    store_rotated(m, out_0, QUERY)
-                store_rotated(m, out_1, KEY)
+                    add_products(m, slice(0, 2 * HEADS), nc.gpsimd)

@@ -232,25 +232,33 @@ def tile_causalselfattention_pa_t_kernel(
                 products[r] = prod_new
             return products[r][:, HEADS * s : HEADS * (s + 1)]
 
+        HALF_ROUNDS = (slice(0, TILES // 2), slice(TILES // 2, TILES))
+
         def times_cos(r, s):
             b, places = round_place(r)
-            nc.vector.tensor_tensor(
-                out=product_tile(r, s, prod_cos, "prod_cos").rearrange("p h j d -> p j h d"),
-                in0=banks[(r, s)][:].rearrange("p j (h d) -> p j h d", h=HEADS),
-                in1=cos_sb[:, places, :].unsqueeze(2).to_broadcast([P, TILES, HEADS, HEAD_DIM]),
-                op=ALU.mult,
-            )
+            target = product_tile(r, s, prod_cos, "prod_cos")
+            for tiles in HALF_ROUNDS:
+                nc.vector.tensor_tensor(
+                    out=target[:, :, tiles, :].rearrange("p h j d -> p j h d"),
+                    in0=banks[(r, s)][:, tiles, :].rearrange("p j (h d) -> p j h d", h=HEADS),
+                    in1=cos_sb[:, places, :][:, tiles, :]
+                    .unsqueeze(2)
+                    .to_broadcast([P, TILES // 2, HEADS, HEAD_DIM]),
+                    op=ALU.mult,
+                )
 
         def times_sin(r, s):
             b, places = round_place(r)
-            halves = banks[(r, s)][:].rearrange("p j (h f i) -> p j h f i", h=HEADS, f=2)
-            table = sin_sb[:, places, :].rearrange("p j (f i) -> p j f i", f=2)
-            nc.vector.tensor_tensor(
-                out=product_tile(r, s, prod_sin, "prod_sin").rearrange("p h j (f i) -> p j h f i", f=2),
-                in0=halves[:, :, :, ::-1, :],
-                in1=table.unsqueeze(2).to_broadcast([P, TILES, HEADS, 2, HALF]),
-                op=ALU.mult,
-            )
+            target = product_tile(r, s, prod_sin, "prod_sin")
+            for tiles in HALF_ROUNDS:
+                halves = banks[(r, s)][:, tiles, :].rearrange("p j (h f i) -> p j h f i", h=HEADS, f=2)
+                table = sin_sb[:, places, :][:, tiles, :].rearrange("p j (f i) -> p j f i", f=2)
+                nc.vector.tensor_tensor(
+                    out=target[:, :, tiles, :].rearrange("p h j (f i) -> p j h f i", f=2),
+                    in0=halves[:, :, :, ::-1, :],
+                    in1=table.unsqueeze(2).to_broadcast([P, TILES // 2, HEADS, 2, HALF]),
+                    op=ALU.mult,
+                )
 
         def add_products(r, pairs, engine):
             b, places = round_place(r)

from contextlib import ExitStack

import concourse.mybir as mybir
from concourse.masks import make_identity

F32 = mybir.dt.float32
BF16 = mybir.dt.bfloat16
I32 = mybir.dt.int32
U32 = mybir.dt.uint32
U8 = mybir.dt.uint8
FP8X4 = mybir.dt.float8_e4m3fn_x4
FP4X4 = mybir.dt.float4_e2m1fn_x4
ALU = mybir.AluOpType
ACT = mybir.ActivationFunctionType

P = 128
BATCH, SEQ, K = 4, 2048, 512
HEADS, HEAD_DIM = 2, 64
HALF = HEAD_DIM // 2
FEATURES = 3 * HEADS * HEAD_DIM
STREAMS = FEATURES // P
QUERY, KEY, VALUE = 0, 1, 2
TOKENS_PER_PARTITION = SEQ // P
TILES = 4
ROUND_TOKENS = TILES * P
TURNED = 3
ROUNDS_PER_BATCH = TOKENS_PER_PARTITION // TILES
ROUNDS = BATCH * ROUNDS_PER_BATCH
WORDS = K // 2
WARM_UPS = 4

FLOPS = 2 * BATCH * SEQ * K * FEATURES


def tile_causalselfattention_pa_t_kernel(
    tc, x, rope_cos, rope_sin, qkv_w_words, qkv_w_scales, qkv_b, out_0, out_1, out_2
):
    nc = tc.nc
    with ExitStack() as ctx:
        ctx.enter_context(tc.manual_schedule())
        const = ctx.enter_context(tc.tile_pool(name="const", bufs=1))
        x_pool = ctx.enter_context(tc.tile_pool(name="x", bufs=BATCH))
        quant_pool = ctx.enter_context(tc.tile_pool(name="quant", bufs=3))
        grouped_pool = ctx.enter_context(tc.tile_pool(name="grouped", bufs=3))
        feat_pool = ctx.enter_context(tc.tile_pool(name="feat", bufs=2 * STREAMS))
        prod_pool = ctx.enter_context(tc.tile_pool(name="prod", bufs=2))
        out_pool = ctx.enter_context(tc.tile_pool(name="out", bufs=2))
        psum_xt = ctx.enter_context(tc.psum_pool(name="psum_xt", bufs=2))
        psum_acc = ctx.enter_context(tc.psum_pool(name="psum_acc", bufs=STREAMS))
        psum_tok = ctx.enter_context(tc.psum_pool(name="psum_tok", bufs=1))

        def round_place(r):
            b, jq = divmod(r, ROUNDS_PER_BATCH)
            return b, slice(TILES * jq, TILES * (jq + 1))

        x_tiles = []
        for b in range(BATCH):
            x_sb = x_pool.tile([P, TOKENS_PER_PARTITION, K], BF16, tag="x")
            x_tiles.append(x_sb)

        def load_x(b, first, count):
            rows = x[b].rearrange("(p j) k -> p j k", j=TOKENS_PER_PARTITION)
            nc.sync.dma_start(
                out=x_tiles[b][:, first : first + count, :], in_=rows[:, first : first + count, :]
            )

        w_scales = const.tile([P, STREAMS, P], U8, align_bytes=64)
        scale_words = w_scales[:].rearrange("p s c -> p (s c)").bitcast(I32)
        nc.vector.memset(scale_words, 0)

        zeros = const.tile([P, P], BF16)
        nc.vector.memset(zeros[:], 0.0)
        unread = psum_tok.tile([P, TILES, P], F32, tag="tok_value")
        for repeat in range(WARM_UPS):
            nc.tensor.matmul(
                out=unread[:],
                lhsT=zeros[:],
                rhs=zeros[:].unsqueeze(1).to_broadcast([P, TILES, P]),
                start=True,
                stop=True,
            )

        bias_rows = const.tile([P, P], BF16)
        nc.vector.memset(bias_rows[:], 0.0)
        load_x(0, 0, 2)
        load_x(0, 2, 2)

        w_words = const.tile([P, STREAMS, 2 * P], U8, align_bytes=64)
        nc.sync.dma_start(
            out=w_words[:].rearrange("p s c -> p (s c)").bitcast(I32), in_=qkv_w_words[0].bitcast(I32)
        )
        for quadrant in range(4):
            nc.sync.dma_start(
                out=scale_words[32 * quadrant : 32 * quadrant + 4, :],
                in_=qkv_w_scales[0, 4 * quadrant : 4 * quadrant + 4, :].bitcast(I32),
            )
        load_x(0, TILES, TILES)

        cos_sb = const.tile([P, TOKENS_PER_PARTITION, HEAD_DIM], BF16)
        sin_sb = const.tile([P, TOKENS_PER_PARTITION, HEAD_DIM], BF16)
        nc.sync.dma_start(
            out=cos_sb[:], in_=rope_cos[0, 0].rearrange("(p j) d -> p j d", j=TOKENS_PER_PARTITION)
        )
        nc.sync.dma_start(
            out=sin_sb[:], in_=rope_sin[0, 0].rearrange("(p j) d -> p j d", j=TOKENS_PER_PARTITION)
        )
        load_x(0, 2 * TILES, TILES)
        load_x(0, 3 * TILES, TILES)
        for b in range(1, BATCH):
            load_x(b, 0, TOKENS_PER_PARTITION)

        def negate_sin():
            nc.vector.tensor_scalar(
                out=sin_sb[:, :, 0:HALF], in0=sin_sb[:, :, 0:HALF], scalar1=-1.0, scalar2=None, op0=ALU.mult
            )

        identity = const.tile([P, P], F32)
        make_identity(nc, identity[:])
        nc.gpsimd.dma_start(out=bias_rows[0:STREAMS, :], in_=qkv_b.rearrange("(o c) -> o c", o=STREAMS))

        banks = {}
        bias_rows_f32 = const.tile([P, P], F32)
        bias = const.tile([P, STREAMS], F32)
        value_bias = const.tile([P, P], F32)

        def widen_bias():
            nc.vector.tensor_copy(out=bias_rows_f32[:], in_=bias_rows[:])

        def bias_onto_partitions():
            bias_bank = psum_tok.tile([P, P], F32, tag="tok_value")
            nc.tensor.transpose(out=bias_bank[:], in_=bias_rows_f32[:], identity=identity[:])
            nc.vector.tensor_copy(out=bias[:], in_=bias_bank[:, 0:STREAMS])

        def turn_value_bias():
            value_bank = psum_tok.tile([P, P], F32, tag="tok_value")
            banks["bias"] = value_bank
            nc.tensor.transpose(
                out=value_bank[:],
                in_=bias[:, VALUE : VALUE + 1].to_broadcast([P, P]),
                identity=identity[:],
            )

        def copy_value_bias():
            nc.vector.tensor_copy(out=value_bias[:], in_=banks["bias"][:])

        grouped_tiles = {}
        x_codes = {}
        x_scales = {}

        def transpose_x(r, half_round):
            if half_round == 0:
                grouped_new = grouped_pool.tile([P, 4 * ROUND_TOKENS], BF16, align_bytes=64, tag="grouped")
                grouped_tiles[r] = grouped_new
            b, places = round_place(r)
            x_words = x_tiles[b][:].bitcast(F32)
            grouped_words = grouped_tiles[r][:].bitcast(F32)
            xt = psum_xt.tile([P, 2, 2 * P], F32, tag="xt")
            for tile_in_bank in range(2):
                jj = 2 * half_round + tile_in_bank
                for parity in range(2):
                    nc.tensor.transpose(
                        out=xt[:, parity, P * tile_in_bank : P * (tile_in_bank + 1)],
                        in_=x_words[:, places.start + jj, parity:WORDS:2],
                        identity=identity[:],
                    )
            copy_out = nc.vector.tensor_copy if (r, half_round) == (0, 1) else nc.scalar.copy
            copy_out(
                out=grouped_words[:, 4 * P * half_round : 4 * P * (half_round + 1)].rearrange(
                    "p (n u) -> p n u", u=2
                ),
                in_=xt[:].rearrange("p u n -> p n u"),
            )

        def quantise(r):
            codes = quant_pool.tile([P, ROUND_TOKENS], U32, align_bytes=64, tag="codes")
            scales = quant_pool.tile([P, ROUND_TOKENS], U8, align_bytes=64, tag="scales")
            nc.vector.quantize_mx(
                out=codes[:].bitcast(FP8X4), scales=scales[:], in_=grouped_tiles[r][:]
            )
            x_codes[r] = codes
            x_scales[r] = scales

        features = {}

        def multiply_w(acc, r, s, first, tokens):
            nc.tensor.matmul_mx(
                out=acc[:, first : first + tokens],
                lhsT=w_words[:, s, :].bitcast(FP4X4),
                lhsT_scale=w_scales[:, s, :],
                rhs=x_codes[r][:, first : first + tokens].bitcast(FP8X4),
                rhs_scale=x_scales[r][:, first : first + tokens],
                start=True,
                stop=True,
            )

        def project(r, operands):
            for s in operands:
                acc = psum_acc.tile([P, ROUND_TOKENS], F32, tag="acc")
                if s == VALUE:
                    multiply_w(acc, r, s, 0, 2 * P)
                    multiply_w(acc, r, s, 2 * P, P)
                else:
                    multiply_w(acc, r, s, 0, ROUND_TOKENS)
                tokens = TURNED * P if s == VALUE else ROUND_TOKENS
                feat = feat_pool.tile([P, ROUND_TOKENS], F32, tag="feat")
                nc.scalar.activation(
                    out=feat[:, 0:tokens],
                    in_=acc[:, 0:tokens],
                    func=ACT.Identity,
                    bias=bias[:, s : s + 1],
                    scale=1.0,
                )
                features[(r, s)] = feat

        prod_cos = {}
        prod_sin = {}
        rotated_tiles = {}

        def back_rotated(r, s):
            tok = psum_tok.tile([P, TILES, P], F32, tag="tok_query" if s == QUERY else "tok_key")
            for jj in range(TILES):
                nc.tensor.transpose(
                    out=tok[:, jj, :],
                    in_=features[(r, s)][:, P * jj : P * (jj + 1)],
                    identity=identity[:],
                )
            banks[(r, s)] = tok

        def product_tile(r, s, products, tag):
            if s == QUERY:
                prod_new = prod_pool.tile([P, 2 * HEADS, TILES, HEAD_DIM], F32, tag=tag)
                products[r] = prod_new
            return products[r][:, HEADS * s : HEADS * (s + 1)]

        HALF_ROUNDS = (slice(0, TILES // 2), slice(TILES // 2, TILES))

        def times_cos(r, s):
            b, places = round_place(r)
            target = product_tile(r, s, prod_cos, "prod_cos")
            for tiles in HALF_ROUNDS:
                nc.vector.tensor_tensor(
                    out=target[:, :, tiles, :].rearrange("p h j d -> p j h d"),
                    in0=banks[(r, s)][:, tiles, :].rearrange("p j (h d) -> p j h d", h=HEADS),
                    in1=cos_sb[:, places, :][:, tiles, :]
                    .unsqueeze(2)
                    .to_broadcast([P, TILES // 2, HEADS, HEAD_DIM]),
                    op=ALU.mult,
                )

        def times_sin(r, s):
            b, places = round_place(r)
            target = product_tile(r, s, prod_sin, "prod_sin")
            for tiles in HALF_ROUNDS:
                halves = banks[(r, s)][:, tiles, :].rearrange("p j (h f i) -> p j h f i", h=HEADS, f=2)
                table = sin_sb[:, places, :][:, tiles, :].rearrange("p j (f i) -> p j f i", f=2)
                nc.vector.tensor_tensor(
                    out=target[:, :, tiles, :].rearrange("p h j (f i) -> p j h f i", f=2),
                    in0=halves[:, :, :, ::-1, :],
                    in1=table.unsqueeze(2).to_broadcast([P, TILES // 2, HEADS, 2, HALF]),
                    op=ALU.mult,
                )

        def add_products(r, pairs, engine):
            b, places = round_place(r)
            if places.start == 0 and b not in rotated_tiles:
                rotated_new = out_pool.tile([P, 2 * HEADS, TOKENS_PER_PARTITION, HEAD_DIM], F32, tag="rotated")
                rotated_tiles[b] = rotated_new
            engine.tensor_tensor(
                out=rotated_tiles[b][:, pairs, places, :].rearrange("p g j d -> p g (j d)"),
                in0=prod_cos[r][:, pairs].rearrange("p g j d -> p g (j d)"),
                in1=prod_sin[r][:, pairs].rearrange("p g j d -> p g (j d)"),
                op=ALU.add,
            )

        def store(out, tile_of_batch, r):
            b, places = round_place(r)
            rows = out[b].rearrange("h (p j) d -> p h j d", j=TOKENS_PER_PARTITION)
            if b == BATCH - 1:
                nc.sync.dma_start(out=rows[:, :, places, :], in_=tile_of_batch[:, :, places, :])
            elif places.stop % 8 == 0:
                places = slice(places.stop - 8, places.stop)
                nc.sync.dma_start(out=rows[:, :, places, :], in_=tile_of_batch[:, :, places, :])

        def store_rotated(r, out, s):
            b, places = round_place(r)
            store(out, rotated_tiles[b][:, HEADS * s : HEADS * (s + 1)], r)

        value_tiles = {}

        def back_value(r):
            tok = psum_tok.tile([P, TILES, P], F32, tag="tok_value")
            for jj in range(TURNED):
                nc.tensor.transpose(
                    out=tok[:, jj, :],
                    in_=features[(r, VALUE)][:, P * jj : P * (jj + 1)],
                    identity=identity[:],
                )
            for jj in range(TURNED, TILES):
                nc.tensor.matmul_mx(
                    out=tok[:, jj, :],
                    lhsT=x_codes[r][:, P * jj : P * (jj + 1)].bitcast(FP8X4),
                    lhsT_scale=x_scales[r][:, P * jj : P * (jj + 1)],
                    rhs=w_words[:, VALUE, :].bitcast(FP4X4),
                    rhs_scale=w_scales[:, VALUE, :],
                    start=True,
                    stop=True,
                )
            b, places = round_place(r)
            if places.start == 0:
                value_new = out_pool.tile([P, HEADS, TOKENS_PER_PARTITION, HEAD_DIM], F32, tag="value")
                value_tiles[b] = value_new
            value = value_tiles[b][:, :, places, :]
            nc.scalar.copy(
                out=value[:, :, 0:TURNED, :].rearrange("p h j d -> p j h d"),
                in_=tok[:, 0:TURNED, :].rearrange("p j (h d) -> p j h d", h=HEADS),
            )
            banks[(r, VALUE)] = tok

        def add_value_bias_and_store(r):
            b, places = round_place(r)
            nc.vector.tensor_tensor(
                out=value_tiles[b][:, :, places.start + TURNED : places.stop, :].rearrange("p h j d -> p j h d"),
                in0=banks[(r, VALUE)][:, TURNED:TILES, :].rearrange("p j (h d) -> p j h d", h=HEADS),
                in1=value_bias[:]
                .rearrange("p (h d) -> p h d", h=HEADS)
                .unsqueeze(1)
                .to_broadcast([P, TILES - TURNED, HEADS, HEAD_DIM]),
                op=ALU.add,
            )
            store(out_2, value_tiles[b][:], r)

        def live(r):
            return 0 <= r < ROUNDS

        last = ROUNDS - 1
        for m in range(-3, ROUNDS):
            if live(m + 1):
                quantise(m + 1)
            if m == -1:
                bias_onto_partitions()
                negate_sin()
            if m == 0:
                copy_value_bias()
            if live(m):
                times_cos(m, QUERY)
                times_sin(m, QUERY)
                back_rotated(m, KEY)
                back_value(m)
            if live(m + 1):
                project(m + 1, (QUERY, KEY, VALUE))
            if m == -1:
                turn_value_bias()
            if m == -2:
                widen_bias()
            if live(m + 3):
                transpose_x(m + 3, 0)
                transpose_x(m + 3, 1)
            if live(m + 1):
                back_rotated(m + 1, QUERY)
            if live(m):
                times_cos(m, KEY)
                add_value_bias_and_store(m)
                if m == last:
                    store_rotated(m - 1, out_1, KEY)
                elif live(m - 1):
                    store_rotated(m - 1, out_0, QUERY)
                    store_rotated(m - 1, out_1, KEY)
                times_sin(m, KEY)
                if m == last:
                    b, places = round_place(m)
                    for pair in range(2 * HEADS):
                        s, h = divmod(pair, HEADS)
                        add_products(m, slice(pair, pair + 1), nc.vector)
                        rows = (out_0, out_1)[s][b, h].rearrange("(p j) d -> p j d", j=TOKENS_PER_PARTITION)
                        nc.sync.dma_start(out=rows[:, places, :], in_=rotated_tiles[b][:, pair, places, :])
                elif m == last - 1:
                    add_products(m, slice(0, HEADS), nc.gpsimd)
                    store_rotated(m, out_0, QUERY)
                    add_products(m, slice(HEADS, 2 * HEADS), nc.gpsimd)
                else:
                    add_products(m, slice(0, 2 * HEADS), nc.gpsimd)
